import numpy as np
import ml_dtypes


def mxq(x, axis, fmt="e4m3"):
    dtype, down = {"e4m3": (ml_dtypes.float8_e4m3fn, 7), "e5m2": (ml_dtypes.float8_e5m2, 14)}[fmt]
    v = np.moveaxis(np.asarray(x, np.float32).astype(ml_dtypes.bfloat16).astype(np.float64), axis, -1)
    blocks = v.reshape(v.shape[:-1] + (-1, 32))
    amax = np.abs(blocks).max(-1, keepdims=True)
    byte = np.maximum(np.where(amax > 0, np.frexp(amax)[1] - 1 + 127, 0) - down, 1)
    scale = np.exp2(byte - 127.0)
    codes = (blocks / scale).astype(np.float32).astype(dtype).astype(np.float64)
    return np.moveaxis((codes * scale).reshape(v.shape), -1, axis)


WIDE = False


def mx_kscale(k):
    if not WIDE:
        return np.ones(k)
    levels = np.array([10, -10, 5, -5, 0])
    a = np.random.permutation(np.resize(levels, k // 512 * 4)).reshape(k // 512, 4)
    idx = np.arange(k)
    return np.exp2(a[idx // 512, idx % 128 // 32])


BF16 = ml_dtypes.bfloat16


def bf(x):
    return np.asarray(x, np.float32).astype(BF16)


def f64(x):
    return np.asarray(x).astype(np.float64)


M, K, N = 1024, 2048, 2048


def softplus(v):
    return np.logaddexp(v, 0.0)


def setup_inputs():
    s = mx_kscale(K)
    w_std0 = np.log(np.expm1(0.5 / np.sqrt(K)))
    return {"x": bf(np.random.standard_normal((M, K)) * s),
            "w_loc": bf(np.random.standard_normal((K, N)) * 0.9 / np.sqrt(K) / s[:, None]),
            "w_std": bf(w_std0 + 0.3 * np.random.standard_normal((K, N))),
            "b_loc": bf(np.random.standard_normal((1, N)) * 0.5),
            "b_std": bf(-1.0 + 0.3 * np.random.standard_normal((1, N))),
            "eps_w": bf(np.random.standard_normal((K, N)) / s[:, None]),
            "eps_b": bf(np.random.standard_normal((1, N)))}


def reference(x, w_loc, w_std, b_loc, b_std, eps_w, eps_b):
    w = f64(w_loc) + softplus(f64(w_std)) * f64(eps_w)
    b = f64(b_loc) + softplus(f64(b_std)) * f64(eps_b)
    return (mxq(f64(x), 1, "e4m3") @ mxq(w, 0, "e4m3")) + b

@@ -1,0 +1,324 @@
+from contextlib import ExitStack
+
+import concourse.mybir as mybir
+from concourse.masks import make_identity
+
+FLOPS = 2 * 1024 * 2048 * 2048
+
+F32 = mybir.dt.float32
+BF16 = mybir.dt.bfloat16
+U32 = mybir.dt.uint32
+I32 = mybir.dt.int32
+U8 = mybir.dt.uint8
+FP8X4 = mybir.dt.float8_e4m3fn_x4
+ACT = mybir.ActivationFunctionType
+ALU = mybir.AluOpType
+P = 128
+SIGN_BITS = -0x7FFF8000
+TILES = 16
+
+
+def tile_bayesiandenselayer_kernel(tc, x, w_loc, w_std, b_loc, b_std, eps_w, eps_b, out):
+    nc = tc.nc
+    with ExitStack() as ctx:
+        const = ctx.enter_context(tc.tile_pool(name="const", bufs=1))
+        f32p = ctx.enter_context(tc.tile_pool(name="f32p", bufs=8))
+        stdp = ctx.enter_context(tc.tile_pool(name="stdp", bufs=8))
+        vcp = ctx.enter_context(tc.tile_pool(name="vcp", bufs=4))
+        epsp = ctx.enter_context(tc.tile_pool(name="epsp", bufs=4))
+        locp = ctx.enter_context(tc.tile_pool(name="locp", bufs=4))
+        wbp = ctx.enter_context(tc.tile_pool(name="wbp", bufs=2))
+        wcp = ctx.enter_context(tc.tile_pool(name="wcp", bufs=6))
+        otp = ctx.enter_context(tc.tile_pool(name="otp", bufs=8))
+        ostp = ctx.enter_context(tc.tile_pool(name="ostp", bufs=8))
+        psum = ctx.enter_context(tc.psum_pool(name="psum", bufs=8))
+        ctx.enter_context(tc.manual_schedule())
+
+        ident = const.tile([P, P], F32, name="ident")
+        identb = const.tile([P, P], BF16, name="identb")
+        make_identity(nc, ident[:])
+        make_identity(nc, identb[:])
+        bias_bc = const.tile([P, 256], F32, name="bias_bc")
+        x_codes = const.tile([P, 4, 1024], U32, name="x_codes", align_bytes=64)
+        x_scales = const.tile([P, 4, 1024], U8, name="x_scales", align_bytes=64)
+
+        std, eps, loc, vc, fw, wb, wc, wp = {}, {}, {}, {}, {}, {}, {}, {}
+
+        def pieces(i):
+            if i < 12:
+                return 512 * (i // 4), 512, (i % 4,)
+            return 1536 + 256 * ((i - 12) // 2), 256, (2 * (i % 2), 2 * (i % 2) + 1)
+
+        def load(pool, tag, store, src, i):
+            col, wid, cs = pieces(i)
+            t = pool.tile([P, 4 * len(cs), wid], BF16, name="%s%d" % (tag, i), tag=tag)
+            for s, c in enumerate(cs):
+                nc.sync.dma_start(
+                    out=t[:, 4 * s:4 * s + 4, :],
+                    in_=src[c * 512:(c + 1) * 512, col:col + wid].rearrange("(p j) n -> p j n", j=4),
+                )
+            store[i] = t
+
+        def flat(t):
+            return t[:].rearrange("p j n -> p (j n)")
+
+        def clamp(i):
+            vc[i] = vcp.tile([P, 2048], BF16, name="vc%d" % i, tag="vc")
+            nc.vector.tensor_scalar(
+                out=vc[i][:].bitcast(I32), in0=flat(std[i]).bitcast(I32), scalar1=SIGN_BITS, scalar2=None,
+                op0=ALU.bitwise_or,
+            )
+
+        def exp_phase(tiles):
+            for i in tiles:
+                fw[i] = f32p.tile([P, 2048], F32, name="fw%d" % i, tag="f", align_bytes=64)
+                nc.scalar.activation(out=fw[i][:], in_=vc[i][:], func=ACT.Sigmoid)
+
+        def ln_phase(tiles):
+            for i in tiles:
+                nc.scalar.activation(out=fw[i][:], in_=fw[i][:], func=ACT.Ln, bias=1.0, scale=-1.0)
+
+        def take_max(i):
+            nc.vector.scalar_tensor_tensor(
+                out=fw[i][:], in0=flat(std[i]), scalar=0.0, in1=fw[i][:], op0=ALU.max, op1=ALU.subtract
+            )
+            if i + 8 < TILES:
+                load(stdp, "std", std, w_std, i + 8)
+
+        def times_eps(i):
+            nc.vector.tensor_tensor(out=fw[i][:], in0=fw[i][:], in1=flat(eps[i]), op=ALU.mult)
+            if i + 4 < TILES:
+                load(epsp, "eps", eps, eps_w, i + 4)
+
+        def plus_loc(i, parts=None):
+            cs = pieces(i)[2]
+            n = 2048 // len(cs)
+            if i not in wb:
+                wb[i] = wbp.tile([P, 2048], BF16, name="wb%d" % i, tag="wb", align_bytes=64)
+            for s in (range(len(cs)) if parts is None else parts):
+                nc.vector.tensor_tensor(
+                    out=wb[i][:, s * n:(s + 1) * n].rearrange("p (cc i t) -> p cc t i", i=4, t=4),
+                    in0=fw[i][:, s * n:(s + 1) * n].rearrange("p (t cc i) -> p cc t i", t=4, i=4),
+                    in1=loc[i][:, 4 * s:4 * s + 4, :].rearrange("p t (cc i) -> p cc t i", i=4),
+                    op=ALU.add,
+                )
+
+        def next_loc(i):
+            if i + 4 < TILES:
+                load(locp, "loc", loc, w_loc, i + 4)
+
+        def quantise(i, lo=0, hi=512):
+            if i not in wc:
+                wc[i] = wcp.tile([P, 512], U32, name="wc%d" % i, tag="wc", align_bytes=64)
+                wp[i] = wcp.tile([P, 512], U8, name="wp%d" % i, tag="wp", align_bytes=64)
+            nc.vector.quantize_mx(
+                out=wc[i][:, lo:hi].bitcast(FP8X4), scales=wp[i][:, lo:hi], in_=wb[i][:, 4 * lo:4 * hi]
+            )
+
+        zt = const.tile([P, P], BF16, name="zt")
+        nc.vector.memset(zt[:], 0.0)
+
+        xr = x.rearrange("(r p) k -> p r k", p=P)
+        xh = {}
+        for c in range(4):
+            for h, pool, tag in ((0, epsp, "eps"), (1, locp, "loc")):
+                t = pool.tile([P, 4, 512], BF16, name="x%d_%d" % (c, h), tag=tag)
+                nc.sync.dma_start(out=t[:], in_=xr[:, 4 * h:4 * h + 4, c * 512:(c + 1) * 512])
+                xh[(c, h)] = t
+                if c == 0:
+                    load(stdp, "std", std, w_std, h)
+            if c == 1:
+                for i in (2, 3):
+                    load(stdp, "std", std, w_std, i)
+        for k, vec in enumerate((b_loc, b_std, eps_b)):
+            nc.sync.dma_start(out=zt[16 * k:16 * k + 16, :], in_=vec.rearrange("o (i p) -> (o i) p", p=P))
+        for i in (0, 1):
+            load(epsp, "eps", eps, eps_w, i)
+            load(locp, "loc", loc, w_loc, i)
+        for i in (4, 5, 6, 7):
+            load(stdp, "std", std, w_std, i)
+        for i in (2, 3):
+            load(epsp, "eps", eps, eps_w, i)
+            load(locp, "loc", loc, w_loc, i)
+
+        grp = [f32p.tile([P, 2048], F32, name="grp%d" % c, tag="f", align_bytes=64) for c in range(4)]
+
+
+        def quant_x(c):
+            nc.vector.quantize_mx(
+                out=x_codes[:, c, :].bitcast(FP8X4), scales=x_scales[:, c, :], in_=grp[c][:].bitcast(BF16)
+            )
+
+        for c in range(4):
+            for rp in range(4):
+                ps = psum.tile([P, 2, 256], F32, name="xt%d_%d" % (c, rp), tag="bank")
+                for h in range(2):
+                    r = 2 * rp + h
+                    words = xh[(c, r // 4)][:].bitcast(F32)[:, r % 4, :].rearrange("p (q u) -> p u q", u=2)
+                    for u in range(2):
+                        nc.tensor.transpose(ps[:, u, h * P:(h + 1) * P], words[:, u, :], ident[:])
+                dst = grp[c][:].rearrange("p (m u) -> p m u", u=2)[:, rp * 256:(rp + 1) * 256, :]
+                if c < 2:
+                    nc.vector.tensor_copy(out=dst, in_=ps[:].rearrange("p u m -> p m u"))
+                else:
+                    nc.scalar.copy(out=dst, in_=ps[:].rearrange("p u m -> p m u"))
+                if c == 0 and rp % 2 == 1:
+                    clamp(rp // 2)
+            if c == 0:
+                exp_phase((0, 1))
+                ln_phase((0, 1))
+                quant_x(0)
+            if c == 1:
+                clamp(2)
+                clamp(3)
+                quant_x(1)
+
+        psb = psum.tile([P, P], BF16, name="psb", tag="bank")
+        nc.tensor.transpose(psb[:], zt[:], identb[:])
+        bT = const.tile([P, 48], F32, name="bT")
+        bc = const.tile([P, 16], F32, name="bc")
+        bl = const.tile([P, 16], F32, name="bl")
+        bs = const.tile([P, 16], F32, name="bs")
+        bt = const.tile([P, 16], F32, name="bt")
+        b16 = const.tile([P, 16], F32, name="b16")
+
+        def bias_clamp():
+            nc.vector.tensor_copy(out=bT[:], in_=psb[:, 0:48])
+            nc.vector.scalar_tensor_tensor(
+                out=bc[:], in0=bT[:, 16:32], scalar=-1.0, in1=bT[:, 16:32], op0=ALU.mult, op1=ALU.min
+            )
+
+        def bias_finish():
+            nc.vector.scalar_tensor_tensor(
+                out=bs[:], in0=bT[:, 16:32], scalar=0.0, in1=bl[:], op0=ALU.max, op1=ALU.subtract
+            )
+            nc.vector.tensor_tensor(out=bt[:], in0=bs[:], in1=bT[:, 32:48], op=ALU.mult)
+            nc.vector.tensor_tensor(out=b16[:], in0=bt[:], in1=bT[:, 0:16], op=ALU.add)
+            pb = psum.tile([P, 256], F32, name="pb", tag="bank")
+            for s in range(2):
+                nc.tensor.matmul(
+                    out=pb[:, s * P:(s + 1) * P], lhsT=b16[:, 14 + s:15 + s].to_broadcast([P, P]), rhs=ident[:],
+                    start=True, stop=True,
+                )
+            nc.scalar.copy(out=bias_bc[:], in_=pb[:])
+
+        def codes_of(first, c):
+            n = len(pieces(first)[2])
+            i = first + c // n
+            off = (c % n) * pieces(first)[1]
+            return wc[i], wp[i], off
+
+        ot = {}
+
+        def block_out(first):
+            col, wid = pieces(first)[0:2]
+            for nt in range(wid // P):
+                for mh in range(2):
+                    at = psum.tile([P, 512], F32, name="at%d_%d_%d" % (first, nt, mh), tag="bank")
+                    for c in range(4):
+                        words, plane, off = codes_of(first, c)
+                        nc.tensor.matmul_mx(
+                            out=at[:],
+                            lhsT=words[:, off + nt * P:off + (nt + 1) * P].bitcast(FP8X4),
+                            lhsT_scale=plane[:, off + nt * P:off + (nt + 1) * P],
+                            rhs=x_codes[:, c, mh * 512:(mh + 1) * 512].bitcast(FP8X4),
+                            rhs_scale=x_scales[:, c, mh * 512:(mh + 1) * 512],
+                            start=(c == 0),
+                            stop=(c == 3),
+                        )
+                    ot[(nt, mh)] = otp.tile([P, 512], F32, name="ot%d_%d_%d" % (first, nt, mh), tag="ot")
+                    nc.scalar.activation(
+                        out=ot[(nt, mh)][:], in_=at[:], func=ACT.Identity,
+                        bias=b16[:, col // P + nt:col // P + nt + 1], scale=1.0,
+                    )
+
+        def block_back(first):
+            col, wid = pieces(first)[0:2]
+            per = 512 // wid
+            for mb in range(8 // per):
+                tb = psum.tile([P, per, wid], F32, name="tb%d_%d" % (first, mb), tag="bank")
+                for m2 in range(per):
+                    m = mb * per + m2
+                    for nt in range(wid // P):
+                        nc.tensor.transpose(
+                            tb[:, m2, nt * P:(nt + 1) * P], ot[(nt, m // 4)][:, (m % 4) * P:(m % 4 + 1) * P], ident[:]
+                        )
+                ost = ostp.tile([P, per, wid], F32, name="ost%d_%d" % (first, mb), tag="ost")
+                nc.scalar.copy(out=ost[:], in_=tb[:])
+                nc.gpsimd.dma_start(
+                    out=out[mb * per * P:(mb + 1) * per * P, col:col + wid].rearrange("(m2 p) n -> p m2 n", p=P),
+                    in_=ost[:],
+                )
+
+        acc = {}
+
+        def direct_passes(c):
+            words, plane, off = codes_of(14, c)
+            for m in range(8):
+                if c == 0:
+                    acc[m] = psum.tile([P, 256], F32, name="acc%d" % m, tag="bank")
+                nc.tensor.matmul_mx(
+                    out=acc[m][:],
+                    lhsT=x_codes[:, c, m * P:(m + 1) * P].bitcast(FP8X4),
+                    lhsT_scale=x_scales[:, c, m * P:(m + 1) * P],
+                    rhs=words[:, off:off + 256].bitcast(FP8X4),
+                    rhs_scale=plane[:, off:off + 256],
+                    start=(c == 0),
+                    stop=(c == 3),
+                )
+
+        phase_after = {0: (4, 5, 6, 7), 1: (8, 9, 10, 11), 3: (12, 13, 14, 15)}
+        block_after = {1: 0, 3: 4, 5: 8, 6: 12}
+        for q in range(7):
+            pair = (2 * q, 2 * q + 1)
+            for i in pair:
+                take_max(i)
+            if q == 1:
+                bias_finish()
+            for i in pair:
+                times_eps(i)
+            if q == 0:
+                bias_clamp()
+                exp_phase((2, 3))
+                nc.scalar.activation(out=bl[:], in_=bc[:], func=ACT.Sigmoid)
+                nc.scalar.activation(out=bl[:], in_=bl[:], func=ACT.Ln, bias=1.0, scale=-1.0)
+                ln_phase((2, 3))
+                quant_x(2)
+                quant_x(3)
+            for i in pair:
+                plus_loc(i)
+                next_loc(i)
+            nxt = phase_after.get(q, ())
+            for i in nxt:
+                clamp(i)
+            exp_phase(nxt)
+            if q == 0:
+                ln_phase(nxt)
+            for i in pair:
+                quantise(i)
+            if q in block_after:
+                block_out(block_after[q])
+                ln_phase(nxt)
+                block_back(block_after[q])
+
+        take_max(14)
+        take_max(15)
+        times_eps(14)
+        times_eps(15)
+        plus_loc(14)
+        plus_loc(15, parts=(0,))
+        quantise(14)
+        direct_passes(0)
+        direct_passes(1)
+        plus_loc(15, parts=(1,))
+        quantise(15, 0, 256)
+        direct_passes(2)
+        quantise(15, 256, 512)
+        direct_passes(3)
+        for mb in range(4):
+            ost = ostp.tile([P, 2, 256], F32, name="ostd%d" % mb, tag="ost")
+            for m2 in range(2):
+                nc.vector.tensor_tensor(out=ost[:, m2, :], in0=acc[2 * mb + m2][:], in1=bias_bc[:], op=ALU.add)
+            nc.sync.dma_start(
+                out=out[2 * mb * P:(2 * mb + 2) * P, 1792:2048].rearrange("(m2 p) n -> p m2 n", p=P), in_=ost[:]
+            )

@@ -8,13 +8,12 @@ FLOPS = 2 * 1024 * 2048 * 2048
 F32 = mybir.dt.float32
 BF16 = mybir.dt.bfloat16
 U32 = mybir.dt.uint32
-I32 = mybir.dt.int32
 U8 = mybir.dt.uint8
 FP8X4 = mybir.dt.float8_e4m3fn_x4
 ACT = mybir.ActivationFunctionType
 ALU = mybir.AluOpType
 P = 128
-SIGN_BITS = -0x7FFF8000
+TINY = 2.0 ** -60
 TILES = 16
 
 
@@ -24,7 +23,6 @@ def tile_bayesiandenselayer_kernel(tc, x, w_loc, w_std, b_loc, b_std, eps_w, eps
         const = ctx.enter_context(tc.tile_pool(name="const", bufs=1))
         f32p = ctx.enter_context(tc.tile_pool(name="f32p", bufs=8))
         stdp = ctx.enter_context(tc.tile_pool(name="stdp", bufs=8))
-        vcp = ctx.enter_context(tc.tile_pool(name="vcp", bufs=4))
         epsp = ctx.enter_context(tc.tile_pool(name="epsp", bufs=4))
         locp = ctx.enter_context(tc.tile_pool(name="locp", bufs=4))
         wbp = ctx.enter_context(tc.tile_pool(name="wbp", bufs=2))
@@ -42,7 +40,7 @@ def tile_bayesiandenselayer_kernel(tc, x, w_loc, w_std, b_loc, b_std, eps_w, eps
         x_codes = const.tile([P, 4, 1024], U32, name="x_codes", align_bytes=64)
         x_scales = const.tile([P, 4, 1024], U8, name="x_scales", align_bytes=64)
 
-        std, eps, loc, vc, fw, wb, wc, wp = {}, {}, {}, {}, {}, {}, {}, {}
+        std, eps, loc, fw, wb, wc, wp = {}, {}, {}, {}, {}, {}, {}
 
         def pieces(i):
             if i < 12:
@@ -62,25 +60,18 @@ def tile_bayesiandenselayer_kernel(tc, x, w_loc, w_std, b_loc, b_std, eps_w, eps
         def flat(t):
             return t[:].rearrange("p j n -> p (j n)")
 
-        def clamp(i):
-            vc[i] = vcp.tile([P, 2048], BF16, name="vc%d" % i, tag="vc")
-            nc.vector.tensor_scalar(
-                out=vc[i][:].bitcast(I32), in0=flat(std[i]).bitcast(I32), scalar1=SIGN_BITS, scalar2=None,
-                op0=ALU.bitwise_or,
-            )
-
         def exp_phase(tiles):
             for i in tiles:
                 fw[i] = f32p.tile([P, 2048], F32, name="fw%d" % i, tag="f", align_bytes=64)
-                nc.scalar.activation(out=fw[i][:], in_=vc[i][:], func=ACT.Sigmoid)
+                nc.scalar.activation(out=fw[i][:], in_=flat(std[i]), func=ACT.Sigmoid, scale=-1.0)
 
         def ln_phase(tiles):
             for i in tiles:
-                nc.scalar.activation(out=fw[i][:], in_=fw[i][:], func=ACT.Ln, bias=1.0, scale=-1.0)
+                nc.scalar.activation(out=fw[i][:], in_=fw[i][:], func=ACT.Ln, bias=TINY)
 
         def take_max(i):
             nc.vector.scalar_tensor_tensor(
-                out=fw[i][:], in0=flat(std[i]), scalar=0.0, in1=fw[i][:], op0=ALU.max, op1=ALU.subtract
+                out=fw[i][:], in0=fw[i][:], scalar=-1.0, in1=flat(std[i]), op0=ALU.mult, op1=ALU.max
             )
             if i + 8 < TILES:
                 load(stdp, "std", std, w_std, i + 8)
@@ -162,21 +153,16 @@ def tile_bayesiandenselayer_kernel(tc, x, w_loc, w_std, b_loc, b_std, eps_w, eps
                     nc.vector.tensor_copy(out=dst, in_=ps[:].rearrange("p u m -> p m u"))
                 else:
                     nc.scalar.copy(out=dst, in_=ps[:].rearrange("p u m -> p m u"))
-                if c == 0 and rp % 2 == 1:
-                    clamp(rp // 2)
             if c == 0:
                 exp_phase((0, 1))
                 ln_phase((0, 1))
                 quant_x(0)
             if c == 1:
-                clamp(2)
-                clamp(3)
                 quant_x(1)
 
         psb = psum.tile([P, P], BF16, name="psb", tag="bank")
         nc.tensor.transpose(psb[:], zt[:], identb[:])
         bT = const.tile([P, 48], F32, name="bT")
-        bc = const.tile([P, 16], F32, name="bc")
         bl = const.tile([P, 16], F32, name="bl")
         bs = const.tile([P, 16], F32, name="bs")
         bt = const.tile([P, 16], F32, name="bt")
@@ -184,13 +170,10 @@ def tile_bayesiandenselayer_kernel(tc, x, w_loc, w_std, b_loc, b_std, eps_w, eps
 
         def bias_clamp():
             nc.vector.tensor_copy(out=bT[:], in_=psb[:, 0:48])
-            nc.vector.scalar_tensor_tensor(
-                out=bc[:], in0=bT[:, 16:32], scalar=-1.0, in1=bT[:, 16:32], op0=ALU.mult, op1=ALU.min
-            )
 
         def bias_finish():
             nc.vector.scalar_tensor_tensor(
-                out=bs[:], in0=bT[:, 16:32], scalar=0.0, in1=bl[:], op0=ALU.max, op1=ALU.subtract
+                out=bs[:], in0=bl[:], scalar=-1.0, in1=bT[:, 16:32], op0=ALU.mult, op1=ALU.max
             )
             nc.vector.tensor_tensor(out=bt[:], in0=bs[:], in1=bT[:, 32:48], op=ALU.mult)
             nc.vector.tensor_tensor(out=b16[:], in0=bt[:], in1=bT[:, 0:16], op=ALU.add)
@@ -280,8 +263,8 @@ def tile_bayesiandenselayer_kernel(tc, x, w_loc, w_std, b_loc, b_std, eps_w, eps
             if q == 0:
                 bias_clamp()
                 exp_phase((2, 3))
-                nc.scalar.activation(out=bl[:], in_=bc[:], func=ACT.Sigmoid)
-                nc.scalar.activation(out=bl[:], in_=bl[:], func=ACT.Ln, bias=1.0, scale=-1.0)
+                nc.scalar.activation(out=bl[:], in_=bT[:, 16:32], func=ACT.Sigmoid, scale=-1.0)
+                nc.scalar.activation(out=bl[:], in_=bl[:], func=ACT.Ln, bias=TINY)
                 ln_phase((2, 3))
                 quant_x(2)
                 quant_x(3)
@@ -289,8 +272,6 @@ def tile_bayesiandenselayer_kernel(tc, x, w_loc, w_std, b_loc, b_std, eps_w, eps
                 plus_loc(i)
                 next_loc(i)
             nxt = phase_after.get(q, ())
-            for i in nxt:
-                clamp(i)
             exp_phase(nxt)
             if q == 0:
                 ln_phase(nxt)

@@ -192,6 +192,12 @@ def tile_bayesiandenselayer_kernel(tc, x, w_loc, w_std, b_loc, b_std, eps_w, eps
             return wc[i], wp[i], off
 
         ot = {}
+        pending = []
+
+        def flush():
+            for dst, t in pending:
+                nc.sync.dma_start(out=dst, in_=t[:])
+            pending.clear()
 
         def block_out(first):
             col, wid = pieces(first)[0:2]
@@ -228,9 +234,8 @@ def tile_bayesiandenselayer_kernel(tc, x, w_loc, w_std, b_loc, b_std, eps_w, eps
                         )
                 ost = ostp.tile([P, per, wid], F32, name="ost%d_%d" % (first, mb), tag="ost")
                 nc.scalar.copy(out=ost[:], in_=tb[:])
-                nc.gpsimd.dma_start(
-                    out=out[mb * per * P:(mb + 1) * per * P, col:col + wid].rearrange("(m2 p) n -> p m2 n", p=P),
-                    in_=ost[:],
+                pending.append(
+                    (out[mb * per * P:(mb + 1) * per * P, col:col + wid].rearrange("(m2 p) n -> p m2 n", p=P), ost)
                 )
 
         acc = {}
@@ -251,7 +256,6 @@ def tile_bayesiandenselayer_kernel(tc, x, w_loc, w_std, b_loc, b_std, eps_w, eps
                 )
 
         phase_after = {0: (4, 5, 6, 7), 1: (8, 9, 10, 11), 3: (12, 13, 14, 15)}
-        block_after = {1: 0, 3: 4, 5: 8, 6: 12}
         for q in range(7):
             pair = (2 * q, 2 * q + 1)
             for i in pair:
@@ -260,6 +264,21 @@ def tile_bayesiandenselayer_kernel(tc, x, w_loc, w_std, b_loc, b_std, eps_w, eps
                 bias_finish()
             for i in pair:
                 times_eps(i)
+            if q == 2:
+                block_out(0)
+                ln_phase((8, 9, 10, 11))
+            if q == 3:
+                block_back(0)
+            if q == 4:
+                flush()
+                block_out(4)
+                ln_phase((12, 13, 14, 15))
+            if q == 5:
+                block_back(4)
+            if q == 6:
+                flush()
+                block_back(8)
+                flush()
             if q == 0:
                 bias_clamp()
                 exp_phase((2, 3))
@@ -277,10 +296,12 @@ def tile_bayesiandenselayer_kernel(tc, x, w_loc, w_std, b_loc, b_std, eps_w, eps
                 ln_phase(nxt)
             for i in pair:
                 quantise(i)
-            if q in block_after:
-                block_out(block_after[q])
-                ln_phase(nxt)
-                block_back(block_after[q])
+            if q == 5:
+                block_out(8)
+            if q == 6:
+                block_out(12)
+                block_back(12)
+                flush()
 
         take_max(14)
         take_max(15)

@@ -88,9 +88,9 @@ def tile_bayesiandenselayer_kernel(tc, x, w_loc, w_std, b_loc, b_std, eps_w, eps
                 wb[i] = wbp.tile([P, 2048], BF16, name="wb%d" % i, tag="wb", align_bytes=64)
             for s in (range(len(cs)) if parts is None else parts):
                 nc.vector.tensor_tensor(
-                    out=wb[i][:, s * n:(s + 1) * n].rearrange("p (cc i t) -> p cc t i", i=4, t=4),
-                    in0=fw[i][:, s * n:(s + 1) * n].rearrange("p (t cc i) -> p cc t i", t=4, i=4),
-                    in1=loc[i][:, 4 * s:4 * s + 4, :].rearrange("p t (cc i) -> p cc t i", i=4),
+                    out=wb[i][:, s * n:(s + 1) * n].rearrange("p (cc i t) -> p cc t i", i=8, t=4),
+                    in0=fw[i][:, s * n:(s + 1) * n].rearrange("p (t cc i) -> p cc t i", t=4, i=8),
+                    in1=loc[i][:, 4 * s:4 * s + 4, :].rearrange("p t (cc i) -> p cc t i", i=8),
                     op=ALU.add,
                 )
 

@@ -29,6 +29,8 @@ def tile_bayesiandenselayer_kernel(tc, x, w_loc, w_std, b_loc, b_std, eps_w, eps
         wcp = ctx.enter_context(tc.tile_pool(name="wcp", bufs=6))
         otp = ctx.enter_context(tc.tile_pool(name="otp", bufs=8))
         ostp = ctx.enter_context(tc.tile_pool(name="ostp", bufs=8))
+        xlp = ctx.enter_context(tc.tile_pool(name="xlp", bufs=4))
+        glp = ctx.enter_context(tc.tile_pool(name="glp", bufs=2))
         psum = ctx.enter_context(tc.psum_pool(name="psum", bufs=8))
         ctx.enter_context(tc.manual_schedule())
 
@@ -111,7 +113,7 @@ def tile_bayesiandenselayer_kernel(tc, x, w_loc, w_std, b_loc, b_std, eps_w, eps
 
         xr = x.rearrange("(r p) k -> p r k", p=P)
         xh = {}
-        for c in range(4):
+        for c in range(2):
             for h, pool, tag in ((0, epsp, "eps"), (1, locp, "loc")):
                 t = pool.tile([P, 4, 512], BF16, name="x%d_%d" % (c, h), tag=tag)
                 nc.sync.dma_start(out=t[:], in_=xr[:, 4 * h:4 * h + 4, c * 512:(c + 1) * 512])
@@ -131,8 +133,14 @@ def tile_bayesiandenselayer_kernel(tc, x, w_loc, w_std, b_loc, b_std, eps_w, eps
         for i in (2, 3):
             load(epsp, "eps", eps, eps_w, i)
             load(locp, "loc", loc, w_loc, i)
+        for c in (2, 3):
+            for h in range(2):
+                t = xlp.tile([P, 4, 512], BF16, name="x%d_%d" % (c, h), tag="xl")
+                nc.sync.dma_start(out=t[:], in_=xr[:, 4 * h:4 * h + 4, c * 512:(c + 1) * 512])
+                xh[(c, h)] = t
 
-        grp = [f32p.tile([P, 2048], F32, name="grp%d" % c, tag="f", align_bytes=64) for c in range(4)]
+        grp = [f32p.tile([P, 2048], F32, name="grp%d" % c, tag="f", align_bytes=64) for c in range(2)]
+        grp.extend([glp.tile([P, 2048], F32, name="grp%d" % c, tag="gl", align_bytes=64) for c in (2, 3)])
 
 
         def quant_x(c):
@@ -140,7 +148,7 @@ def tile_bayesiandenselayer_kernel(tc, x, w_loc, w_std, b_loc, b_std, eps_w, eps
                 out=x_codes[:, c, :].bitcast(FP8X4), scales=x_scales[:, c, :], in_=grp[c][:].bitcast(BF16)
             )
 
-        for c in range(4):
+        def x_chunk(c):
             for rp in range(4):
                 ps = psum.tile([P, 2, 256], F32, name="xt%d_%d" % (c, rp), tag="bank")
                 for h in range(2):
@@ -153,12 +161,13 @@ def tile_bayesiandenselayer_kernel(tc, x, w_loc, w_std, b_loc, b_std, eps_w, eps
                     nc.vector.tensor_copy(out=dst, in_=ps[:].rearrange("p u m -> p m u"))
                 else:
                     nc.scalar.copy(out=dst, in_=ps[:].rearrange("p u m -> p m u"))
-            if c == 0:
-                exp_phase((0, 1))
-                ln_phase((0, 1))
-                quant_x(0)
-            if c == 1:
-                quant_x(1)
+
+        x_chunk(0)
+        exp_phase((0, 1))
+        ln_phase((0, 1))
+        quant_x(0)
+        x_chunk(1)
+        quant_x(1)
 
         psb = psum.tile([P, P], BF16, name="psb", tag="bank")
         nc.tensor.transpose(psb[:], zt[:], identb[:])
@@ -260,11 +269,15 @@ def tile_bayesiandenselayer_kernel(tc, x, w_loc, w_std, b_loc, b_std, eps_w, eps
             pair = (2 * q, 2 * q + 1)
             for i in pair:
                 take_max(i)
-            if q == 1:
-                bias_finish()
             for i in pair:
                 times_eps(i)
+            if q == 1:
+                x_chunk(2)
+                x_chunk(3)
             if q == 2:
+                quant_x(2)
+                quant_x(3)
+                bias_finish()
                 block_out(0)
                 ln_phase((8, 9, 10, 11))
             if q == 3:
@@ -282,17 +295,15 @@ def tile_bayesiandenselayer_kernel(tc, x, w_loc, w_std, b_loc, b_std, eps_w, eps
             if q == 0:
                 bias_clamp()
                 exp_phase((2, 3))
-                nc.scalar.activation(out=bl[:], in_=bT[:, 16:32], func=ACT.Sigmoid, scale=-1.0)
-                nc.scalar.activation(out=bl[:], in_=bl[:], func=ACT.Ln, bias=TINY)
                 ln_phase((2, 3))
-                quant_x(2)
-                quant_x(3)
             for i in pair:
                 plus_loc(i)
                 next_loc(i)
             nxt = phase_after.get(q, ())
             exp_phase(nxt)
             if q == 0:
+                nc.scalar.activation(out=bl[:], in_=bT[:, 16:32], func=ACT.Sigmoid, scale=-1.0)
+                nc.scalar.activation(out=bl[:], in_=bl[:], func=ACT.Ln, bias=TINY)
                 ln_phase(nxt)
             for i in pair:
                 quantise(i)

@@ -13,24 +13,28 @@ FP8X4 = mybir.dt.float8_e4m3fn_x4
 ACT = mybir.ActivationFunctionType
 ALU = mybir.AluOpType
 P = 128
-TINY = 2.0 ** -60
+CLAMP = 32.0
+TINY = 2.0 ** -63
 TILES = 16
+EPS_BUFS = 6
+STD_BUFS = 6
+LOC_BUFS = 4
 
 
 def tile_bayesiandenselayer_kernel(tc, x, w_loc, w_std, b_loc, b_std, eps_w, eps_b, out):
     nc = tc.nc
     with ExitStack() as ctx:
         const = ctx.enter_context(tc.tile_pool(name="const", bufs=1))
-        f32p = ctx.enter_context(tc.tile_pool(name="f32p", bufs=8))
-        stdp = ctx.enter_context(tc.tile_pool(name="stdp", bufs=8))
-        epsp = ctx.enter_context(tc.tile_pool(name="epsp", bufs=4))
-        locp = ctx.enter_context(tc.tile_pool(name="locp", bufs=4))
+        f32p = ctx.enter_context(tc.tile_pool(name="f32p", bufs=10))
+        stdp = ctx.enter_context(tc.tile_pool(name="stdp", bufs=STD_BUFS))
+        epsp = ctx.enter_context(tc.tile_pool(name="epsp", bufs=EPS_BUFS))
+        grp = ctx.enter_context(tc.tile_pool(name="grp", bufs=2))
+        locp = ctx.enter_context(tc.tile_pool(name="locp", bufs=LOC_BUFS))
         wbp = ctx.enter_context(tc.tile_pool(name="wbp", bufs=2))
         wcp = ctx.enter_context(tc.tile_pool(name="wcp", bufs=6))
         otp = ctx.enter_context(tc.tile_pool(name="otp", bufs=8))
         ostp = ctx.enter_context(tc.tile_pool(name="ostp", bufs=8))
-        xlp = ctx.enter_context(tc.tile_pool(name="xlp", bufs=4))
-        glp = ctx.enter_context(tc.tile_pool(name="glp", bufs=2))
+        xlp = ctx.enter_context(tc.tile_pool(name="xlp", bufs=2))
         psum = ctx.enter_context(tc.psum_pool(name="psum", bufs=8))
         ctx.enter_context(tc.manual_schedule())
 
@@ -42,14 +46,18 @@ def tile_bayesiandenselayer_kernel(tc, x, w_loc, w_std, b_loc, b_std, eps_w, eps
         x_codes = const.tile([P, 4, 1024], U32, name="x_codes", align_bytes=64)
         x_scales = const.tile([P, 4, 1024], U8, name="x_scales", align_bytes=64)
 
-        std, eps, loc, fw, wb, wc, wp = {}, {}, {}, {}, {}, {}, {}
+        std, eps, loc, fw, wb, wc, wp, gr = {}, {}, {}, {}, {}, {}, {}, {}
 
         def pieces(i):
             if i < 12:
                 return 512 * (i // 4), 512, (i % 4,)
-            return 1536 + 256 * ((i - 12) // 2), 256, (2 * (i % 2), 2 * (i % 2) + 1)
+            if i < 14:
+                return 1536, 256, (2 * (i % 2), 2 * (i % 2) + 1)
+            return 1792 + 128 * (i - 14), 128, (0, 1, 2, 3)
 
         def load(pool, tag, store, src, i):
+            if i >= TILES:
+                return
             col, wid, cs = pieces(i)
             t = pool.tile([P, 4 * len(cs), wid], BF16, name="%s%d" % (tag, i), tag=tag)
             for s, c in enumerate(cs):
@@ -59,29 +67,40 @@ def tile_bayesiandenselayer_kernel(tc, x, w_loc, w_std, b_loc, b_std, eps_w, eps
                 )
             store[i] = t
 
+        def load_std(i):
+            load(stdp, "std", std, w_std, i)
+
+        def load_eps(i):
+            load(epsp, "eps", eps, eps_w, i)
+
+        def load_loc(i):
+            load(locp, "loc", loc, w_loc, i)
+
         def flat(t):
             return t[:].rearrange("p j n -> p (j n)")
 
-        def exp_phase(tiles):
+        def sigmoid(tiles):
             for i in tiles:
                 fw[i] = f32p.tile([P, 2048], F32, name="fw%d" % i, tag="f", align_bytes=64)
                 nc.scalar.activation(out=fw[i][:], in_=flat(std[i]), func=ACT.Sigmoid, scale=-1.0)
 
-        def ln_phase(tiles):
+        def ln(tiles):
             for i in tiles:
                 nc.scalar.activation(out=fw[i][:], in_=fw[i][:], func=ACT.Ln, bias=TINY)
 
-        def take_max(i):
-            nc.vector.scalar_tensor_tensor(
-                out=fw[i][:], in0=fw[i][:], scalar=-1.0, in1=flat(std[i]), op0=ALU.mult, op1=ALU.max
+        def grow(i):
+            gr[i] = grp.tile([P, 2048], BF16, name="gr%d" % i, tag="gr")
+            nc.vector.tensor_scalar(
+                out=gr[i][:], in0=flat(std[i]), scalar1=-1.0 / CLAMP, scalar2=-1.0, op0=ALU.mult, op1=ALU.min
             )
-            if i + 8 < TILES:
-                load(stdp, "std", std, w_std, i + 8)
+
+        def grow_eps(i):
+            nc.vector.tensor_tensor(out=flat(eps[i]), in0=flat(eps[i]), in1=gr[i][:], op=ALU.mult)
 
         def times_eps(i):
-            nc.vector.tensor_tensor(out=fw[i][:], in0=fw[i][:], in1=flat(eps[i]), op=ALU.mult)
-            if i + 4 < TILES:
-                load(epsp, "eps", eps, eps_w, i + 4)
+            nc.vector.scalar_tensor_tensor(
+                out=fw[i][:], in0=fw[i][:], scalar=-CLAMP, in1=flat(eps[i]), op0=ALU.max, op1=ALU.mult
+            )
 
         def plus_loc(i, parts=None):
             cs = pieces(i)[2]
@@ -96,10 +115,6 @@ def tile_bayesiandenselayer_kernel(tc, x, w_loc, w_std, b_loc, b_std, eps_w, eps
                     op=ALU.add,
                 )
 
-        def next_loc(i):
-            if i + 4 < TILES:
-                load(locp, "loc", loc, w_loc, i + 4)
-
         def quantise(i, lo=0, hi=512):
             if i not in wc:
                 wc[i] = wcp.tile([P, 512], U32, name="wc%d" % i, tag="wc", align_bytes=64)
@@ -113,72 +128,88 @@ def tile_bayesiandenselayer_kernel(tc, x, w_loc, w_std, b_loc, b_std, eps_w, eps
 
         xr = x.rearrange("(r p) k -> p r k", p=P)
         xh = {}
-        for c in range(2):
-            for h, pool, tag in ((0, epsp, "eps"), (1, locp, "loc")):
-                t = pool.tile([P, 4, 512], BF16, name="x%d_%d" % (c, h), tag=tag)
-                nc.sync.dma_start(out=t[:], in_=xr[:, 4 * h:4 * h + 4, c * 512:(c + 1) * 512])
-                xh[(c, h)] = t
-                if c == 0:
-                    load(stdp, "std", std, w_std, h)
-            if c == 1:
-                for i in (2, 3):
-                    load(stdp, "std", std, w_std, i)
-        for k, vec in enumerate((b_loc, b_std, eps_b)):
-            nc.sync.dma_start(out=zt[16 * k:16 * k + 16, :], in_=vec.rearrange("o (i p) -> (o i) p", p=P))
-        for i in (0, 1):
-            load(epsp, "eps", eps, eps_w, i)
-            load(locp, "loc", loc, w_loc, i)
-        for i in (4, 5, 6, 7):
-            load(stdp, "std", std, w_std, i)
-        for i in (2, 3):
-            load(epsp, "eps", eps, eps_w, i)
-            load(locp, "loc", loc, w_loc, i)
-        for c in (2, 3):
-            for h in range(2):
-                t = xlp.tile([P, 4, 512], BF16, name="x%d_%d" % (c, h), tag="xl")
-                nc.sync.dma_start(out=t[:], in_=xr[:, 4 * h:4 * h + 4, c * 512:(c + 1) * 512])
-                xh[(c, h)] = t
 
-        grp = [f32p.tile([P, 2048], F32, name="grp%d" % c, tag="f", align_bytes=64) for c in range(2)]
-        grp.extend([glp.tile([P, 2048], F32, name="grp%d" % c, tag="gl", align_bytes=64) for c in (2, 3)])
+        def load_x(c, h):
+            pool, tag = ((locp, "loc"), (locp, "loc"), (xlp, "xl"), (stdp, "std"))[c]
+            t = pool.tile([P, 4, 512], BF16, name="x%d_%d" % (c, h), tag=tag)
+            nc.sync.dma_start(out=t[:], in_=xr[:, 4 * h:4 * h + 4, c * 512:(c + 1) * 512])
+            xh[(c, h)] = t
 
+        xg = [f32p.tile([P, 2048], F32, name="xg%d" % c, tag="f", align_bytes=64) for c in range(4)]
 
         def quant_x(c):
             nc.vector.quantize_mx(
-                out=x_codes[:, c, :].bitcast(FP8X4), scales=x_scales[:, c, :], in_=grp[c][:].bitcast(BF16)
+                out=x_codes[:, c, :].bitcast(FP8X4), scales=x_scales[:, c, :], in_=xg[c][:].bitcast(BF16)
             )
 
-        def x_chunk(c):
-            for rp in range(4):
+        def x_half(c, h, copy):
+            for rp in (2 * h, 2 * h + 1):
                 ps = psum.tile([P, 2, 256], F32, name="xt%d_%d" % (c, rp), tag="bank")
-                for h in range(2):
-                    r = 2 * rp + h
-                    words = xh[(c, r // 4)][:].bitcast(F32)[:, r % 4, :].rearrange("p (q u) -> p u q", u=2)
+                for r2 in range(2):
+                    r = 2 * rp + r2
+                    words = xh[(c, h)][:].bitcast(F32)[:, r % 4, :].rearrange("p (q u) -> p u q", u=2)
                     for u in range(2):
-                        nc.tensor.transpose(ps[:, u, h * P:(h + 1) * P], words[:, u, :], ident[:])
-                dst = grp[c][:].rearrange("p (m u) -> p m u", u=2)[:, rp * 256:(rp + 1) * 256, :]
-                if c < 2:
-                    nc.vector.tensor_copy(out=dst, in_=ps[:].rearrange("p u m -> p m u"))
-                else:
-                    nc.scalar.copy(out=dst, in_=ps[:].rearrange("p u m -> p m u"))
+                        nc.tensor.transpose(ps[:, u, r2 * P:(r2 + 1) * P], words[:, u, :], ident[:])
+                dst = xg[c][:].rearrange("p (m u) -> p m u", u=2)[:, rp * 256:(rp + 1) * 256, :]
+                copy(out=dst, in_=ps[:].rearrange("p u m -> p m u"))
 
-        x_chunk(0)
-        exp_phase((0, 1))
-        ln_phase((0, 1))
+        load_std(0)
+        load_x(0, 0)
+        load_std(1)
+        load_x(0, 1)
+        load_std(2)
+        load_eps(0)
+        load_std(3)
+        load_eps(1)
+        load_eps(2)
+        load_std(4)
+        load_eps(3)
+        load_eps(4)
+        load_std(5)
+        for k, vec in enumerate((b_loc, b_std, eps_b)):
+            nc.sync.dma_start(out=zt[16 * k:16 * k + 16, :], in_=vec.rearrange("o (i p) -> (o i) p", p=P))
+        load_eps(5)
+        load_x(1, 0)
+        load_x(1, 1)
+        load_loc(0)
+        load_loc(1)
+        load_x(2, 0)
+        load_x(2, 1)
+
+        grow(0)
+        sigmoid((0,))
+        x_half(0, 0, nc.vector.tensor_copy)
+        grow(1)
+        x_half(0, 1, nc.vector.tensor_copy)
+        grow_eps(0)
         quant_x(0)
-        x_chunk(1)
-        quant_x(1)
+        grow(2)
+        grow_eps(1)
+        grow(3)
+        grow_eps(2)
+        grow(4)
+        grow_eps(3)
+        grow_eps(4)
+        sigmoid((1, 2, 3))
+        ln((0, 1, 2, 3))
 
+        load_x(3, 0)
+        load_x(3, 1)
         psb = psum.tile([P, P], BF16, name="psb", tag="bank")
         nc.tensor.transpose(psb[:], zt[:], identb[:])
+        for c in (1, 2, 3):
+            for h in range(2):
+                x_half(c, h, nc.scalar.copy)
+        load_std(6)
+        load_std(7)
+        load_loc(2)
+        load_loc(3)
+
         bT = const.tile([P, 48], F32, name="bT")
         bl = const.tile([P, 16], F32, name="bl")
         bs = const.tile([P, 16], F32, name="bs")
         bt = const.tile([P, 16], F32, name="bt")
         b16 = const.tile([P, 16], F32, name="b16")
-
-        def bias_clamp():
-            nc.vector.tensor_copy(out=bT[:], in_=psb[:, 0:48])
 
         def bias_finish():
             nc.vector.scalar_tensor_tensor(
@@ -192,7 +223,7 @@ def tile_bayesiandenselayer_kernel(tc, x, w_loc, w_std, b_loc, b_std, eps_w, eps
                     out=pb[:, s * P:(s + 1) * P], lhsT=b16[:, 14 + s:15 + s].to_broadcast([P, P]), rhs=ident[:],
                     start=True, stop=True,
                 )
-            nc.scalar.copy(out=bias_bc[:], in_=pb[:])
+            return pb
 
         def codes_of(first, c):
             n = len(pieces(first)[2])
@@ -201,17 +232,11 @@ def tile_bayesiandenselayer_kernel(tc, x, w_loc, w_std, b_loc, b_std, eps_w, eps
             return wc[i], wp[i], off
 
         ot = {}
-        pending = []
-
-        def flush():
-            for dst, t in pending:
-                nc.sync.dma_start(out=dst, in_=t[:])
-            pending.clear()
 
         def block_out(first):
             col, wid = pieces(first)[0:2]
-            for nt in range(wid // P):
-                for mh in range(2):
+            for mh in range(2):
+                for nt in range(wid // P):
                     at = psum.tile([P, 512], F32, name="at%d_%d_%d" % (first, nt, mh), tag="bank")
                     for c in range(4):
                         words, plane, off = codes_of(first, c)
@@ -243,95 +268,124 @@ def tile_bayesiandenselayer_kernel(tc, x, w_loc, w_std, b_loc, b_std, eps_w, eps
                         )
                 ost = ostp.tile([P, per, wid], F32, name="ost%d_%d" % (first, mb), tag="ost")
                 nc.scalar.copy(out=ost[:], in_=tb[:])
-                pending.append(
-                    (out[mb * per * P:(mb + 1) * per * P, col:col + wid].rearrange("(m2 p) n -> p m2 n", p=P), ost)
+                nc.sync.dma_start(
+                    out=out[mb * per * P:(mb + 1) * per * P, col:col + wid].rearrange("(m2 p) n -> p m2 n", p=P),
+                    in_=ost[:],
                 )
 
-        acc = {}
+        def direct_pass(i, c, m, acc):
+            nc.tensor.matmul_mx(
+                out=acc,
+                lhsT=x_codes[:, c, m * P:(m + 1) * P].bitcast(FP8X4),
+                lhsT_scale=x_scales[:, c, m * P:(m + 1) * P],
+                rhs=wc[i][:, c * P:(c + 1) * P].bitcast(FP8X4),
+                rhs_scale=wp[i][:, c * P:(c + 1) * P],
+                start=(c == 0),
+                stop=(c == 3),
+            )
 
-        def direct_passes(c):
-            words, plane, off = codes_of(14, c)
-            for m in range(8):
-                if c == 0:
-                    acc[m] = psum.tile([P, 256], F32, name="acc%d" % m, tag="bank")
-                nc.tensor.matmul_mx(
-                    out=acc[m][:],
-                    lhsT=x_codes[:, c, m * P:(m + 1) * P].bitcast(FP8X4),
-                    lhsT_scale=x_scales[:, c, m * P:(m + 1) * P],
-                    rhs=words[:, off:off + 256].bitcast(FP8X4),
-                    rhs_scale=plane[:, off:off + 256],
-                    start=(c == 0),
-                    stop=(c == 3),
-                )
-
-        phase_after = {0: (4, 5, 6, 7), 1: (8, 9, 10, 11), 3: (12, 13, 14, 15)}
-        for q in range(7):
+        def pair_steps(q):
             pair = (2 * q, 2 * q + 1)
             for i in pair:
-                take_max(i)
-            for i in pair:
                 times_eps(i)
-            if q == 1:
-                x_chunk(2)
-                x_chunk(3)
-            if q == 2:
-                quant_x(2)
-                quant_x(3)
-                bias_finish()
-                block_out(0)
-                ln_phase((8, 9, 10, 11))
-            if q == 3:
-                block_back(0)
-            if q == 4:
-                flush()
-                block_out(4)
-                ln_phase((12, 13, 14, 15))
-            if q == 5:
-                block_back(4)
-            if q == 6:
-                flush()
-                block_back(8)
-                flush()
-            if q == 0:
-                bias_clamp()
-                exp_phase((2, 3))
-                ln_phase((2, 3))
+                load_eps(i + EPS_BUFS)
             for i in pair:
                 plus_loc(i)
-                next_loc(i)
-            nxt = phase_after.get(q, ())
-            exp_phase(nxt)
-            if q == 0:
-                nc.scalar.activation(out=bl[:], in_=bT[:, 16:32], func=ACT.Sigmoid, scale=-1.0)
-                nc.scalar.activation(out=bl[:], in_=bl[:], func=ACT.Ln, bias=TINY)
-                ln_phase(nxt)
+                load_loc(i + LOC_BUFS)
             for i in pair:
                 quantise(i)
-            if q == 5:
-                block_out(8)
-            if q == 6:
-                block_out(12)
-                block_back(12)
-                flush()
+            if q == 0:
+                grow(5)
+                grow_eps(5)
+            elif q < 6:
+                for i in pair:
+                    grow(i + 4)
+                for i in pair:
+                    grow_eps(i + 4)
 
-        take_max(14)
-        take_max(15)
+        pair_steps(0)
+        nc.vector.tensor_copy(out=bT[:], in_=psb[:, 0:48])
+        sigmoid((4, 5, 6, 7))
+        nc.scalar.activation(out=bl[:], in_=bT[:, 16:32], func=ACT.Sigmoid, scale=-1.0)
+        nc.scalar.activation(out=bl[:], in_=bl[:], func=ACT.Ln, bias=TINY)
+        ln((4, 5, 6, 7))
+        load_std(8)
+        load_std(9)
+        load_std(10)
+        load_std(11)
+        pair_steps(1)
+        load_std(12)
+        load_std(13)
+        for c in (1, 2, 3):
+            quant_x(c)
+        pb = bias_finish()
+        sigmoid((8, 9, 10, 11))
+        nc.scalar.copy(out=bias_bc[:], in_=pb[:])
+        pair_steps(2)
+        load_std(14)
+        load_std(15)
+        sigmoid((12, 13, 14, 15))
+        ln((8, 9))
+        block_out(0)
+        pair_steps(3)
+        ln((10, 11))
+        block_back(0)
+        pair_steps(4)
+        ln((12, 13))
+        block_out(4)
+        pair_steps(5)
+        ln((14, 15))
+        block_back(4)
+        block_out(8)
+        pair_steps(6)
+        block_back(8)
+        block_out(12)
+        block_back(12)
+
         times_eps(14)
         times_eps(15)
         plus_loc(14)
-        plus_loc(15, parts=(0,))
+        plus_loc(15, parts=(0, 1, 2))
         quantise(14)
-        direct_passes(0)
-        direct_passes(1)
-        plus_loc(15, parts=(1,))
+        acc14 = []
+        for mh in range(2):
+            t = psum.tile([P, 4, P], F32, name="accA%d" % mh, tag="bank")
+            for m4 in range(4):
+                for c in range(4):
+                    direct_pass(14, c, 4 * mh + m4, t[:, m4, :])
+            acc14.append(t)
         quantise(15, 0, 256)
-        direct_passes(2)
+        acc15 = {}
+        for m in range(6):
+            acc15[m] = psum.tile([P, P], F32, name="accB%d" % m, tag="bank")
+        for c in (0, 1):
+            for m in range(6):
+                direct_pass(15, c, m, acc15[m][:])
+        plus_loc(15, parts=(3,))
         quantise(15, 256, 512)
-        direct_passes(3)
-        for mb in range(4):
-            ost = ostp.tile([P, 2, 256], F32, name="ostd%d" % mb, tag="ost")
-            for m2 in range(2):
-                nc.vector.tensor_tensor(out=ost[:, m2, :], in0=acc[2 * mb + m2][:], in1=bias_bc[:], op=ALU.add)
+        for c in (2, 3):
+            for m in range(6):
+                direct_pass(15, c, m, acc15[m][:])
+
+        def store(ost, mh, col):
             nc.sync.dma_start(
-                out=out[2 * mb * P:(2 * mb + 2) * P, 1792:2048].rearrange("(m2 p) n -> p m2 n", p=P), in_=ost[:]
+                out=out[4 * mh * P:(4 * mh + 4) * P, col:col + P].rearrange("(m p) n -> p m n", p=P), in_=ost[:]
             )
+
+        for mh in range(2):
+            ost = ostp.tile([P, 4, P], F32, name="ostA%d" % mh, tag="ost")
+            nc.vector.tensor_tensor(
+                out=ost[:], in0=acc14[mh][:], in1=bias_bc[:, 0:P].unsqueeze(1).to_broadcast([P, 4, P]), op=ALU.add
+            )
+            store(ost, mh, 1792)
+        for m in (6, 7):
+            acc15[m] = psum.tile([P, P], F32, name="accB%d" % m, tag="bank")
+            for c in range(4):
+                direct_pass(15, c, m, acc15[m][:])
+        for mh in range(2):
+            ost = ostp.tile([P, 4, P], F32, name="ostB%d" % mh, tag="ost")
+            for m4 in range(4):
+                nc.vector.tensor_tensor(
+                    out=ost[:, m4, :], in0=acc15[4 * mh + m4][:], in1=bias_bc[:, P:2 * P], op=ALU.add
+                )
+            store(ost, mh, 1920)

@@ -16,7 +16,7 @@ P = 128
 CLAMP = 32.0
 TINY = 2.0 ** -63
 TILES = 16
-EPS_BUFS = 6
+EPS_BUFS = 8
 STD_BUFS = 6
 LOC_BUFS = 4
 
@@ -25,16 +25,14 @@ def tile_bayesiandenselayer_kernel(tc, x, w_loc, w_std, b_loc, b_std, eps_w, eps
     nc = tc.nc
     with ExitStack() as ctx:
         const = ctx.enter_context(tc.tile_pool(name="const", bufs=1))
-        f32p = ctx.enter_context(tc.tile_pool(name="f32p", bufs=10))
+        f32p = ctx.enter_context(tc.tile_pool(name="f32p", bufs=11))
         stdp = ctx.enter_context(tc.tile_pool(name="stdp", bufs=STD_BUFS))
         epsp = ctx.enter_context(tc.tile_pool(name="epsp", bufs=EPS_BUFS))
-        grp = ctx.enter_context(tc.tile_pool(name="grp", bufs=2))
         locp = ctx.enter_context(tc.tile_pool(name="locp", bufs=LOC_BUFS))
         wbp = ctx.enter_context(tc.tile_pool(name="wbp", bufs=2))
         wcp = ctx.enter_context(tc.tile_pool(name="wcp", bufs=6))
         otp = ctx.enter_context(tc.tile_pool(name="otp", bufs=8))
         ostp = ctx.enter_context(tc.tile_pool(name="ostp", bufs=8))
-        xlp = ctx.enter_context(tc.tile_pool(name="xlp", bufs=2))
         psum = ctx.enter_context(tc.psum_pool(name="psum", bufs=8))
         ctx.enter_context(tc.manual_schedule())
 
@@ -49,10 +47,10 @@ def tile_bayesiandenselayer_kernel(tc, x, w_loc, w_std, b_loc, b_std, eps_w, eps
         std, eps, loc, fw, wb, wc, wp, gr = {}, {}, {}, {}, {}, {}, {}, {}
 
         def pieces(i):
-            if i < 12:
+            if i < 8:
                 return 512 * (i // 4), 512, (i % 4,)
             if i < 14:
-                return 1536, 256, (2 * (i % 2), 2 * (i % 2) + 1)
+                return 256 * (i // 2), 256, (2 * (i % 2), 2 * (i % 2) + 1)
             return 1792 + 128 * (i - 14), 128, (0, 1, 2, 3)
 
         def load(pool, tag, store, src, i):
@@ -89,7 +87,7 @@ def tile_bayesiandenselayer_kernel(tc, x, w_loc, w_std, b_loc, b_std, eps_w, eps
                 nc.scalar.activation(out=fw[i][:], in_=fw[i][:], func=ACT.Ln, bias=TINY)
 
         def grow(i):
-            gr[i] = grp.tile([P, 2048], BF16, name="gr%d" % i, tag="gr")
+            gr[i] = wbp.tile([P, 2048], BF16, name="gr%d" % i, tag="wb", align_bytes=64)
             nc.vector.tensor_scalar(
                 out=gr[i][:], in0=flat(std[i]), scalar1=-1.0 / CLAMP, scalar2=-1.0, op0=ALU.mult, op1=ALU.min
             )
@@ -130,12 +128,16 @@ def tile_bayesiandenselayer_kernel(tc, x, w_loc, w_std, b_loc, b_std, eps_w, eps
         xh = {}
 
         def load_x(c, h):
-            pool, tag = ((locp, "loc"), (locp, "loc"), (xlp, "xl"), (stdp, "std"))[c]
+            pool, tag = ((locp, "loc"), (locp, "loc"), (stdp, "std"), (stdp, "std"))[c]
             t = pool.tile([P, 4, 512], BF16, name="x%d_%d" % (c, h), tag=tag)
             nc.sync.dma_start(out=t[:], in_=xr[:, 4 * h:4 * h + 4, c * 512:(c + 1) * 512])
             xh[(c, h)] = t
 
-        xg = [f32p.tile([P, 2048], F32, name="xg%d" % c, tag="f", align_bytes=64) for c in range(4)]
+        xg = {}
+
+        def x_room(cs):
+            for c in cs:
+                xg[c] = f32p.tile([P, 2048], F32, name="xg%d" % c, tag="f", align_bytes=64)
 
         def quant_x(c):
             nc.vector.quantize_mx(
@@ -153,19 +155,23 @@ def tile_bayesiandenselayer_kernel(tc, x, w_loc, w_std, b_loc, b_std, eps_w, eps
                 dst = xg[c][:].rearrange("p (m u) -> p m u", u=2)[:, rp * 256:(rp + 1) * 256, :]
                 copy(out=dst, in_=ps[:].rearrange("p u m -> p m u"))
 
-        load_std(0)
-        load_x(0, 0)
+        std[0] = stdp.tile([P, 4, 512], BF16, name="std0", tag="std")
+        for j in (0, 2):
+            nc.sync.dma_start(
+                out=std[0][:, j:j + 2, :], in_=w_std[0:512, 0:512].rearrange("(p j) n -> p j n", j=4)[:, j:j + 2, :]
+            )
         load_std(1)
-        load_x(0, 1)
+        load_x(0, 0)
         load_std(2)
+        load_x(0, 1)
         load_eps(0)
         load_std(3)
         load_eps(1)
-        load_eps(2)
         load_std(4)
+        load_eps(2)
+        load_std(5)
         load_eps(3)
         load_eps(4)
-        load_std(5)
         for k, vec in enumerate((b_loc, b_std, eps_b)):
             nc.sync.dma_start(out=zt[16 * k:16 * k + 16, :], in_=vec.rearrange("o (i p) -> (o i) p", p=P))
         load_eps(5)
@@ -173,37 +179,45 @@ def tile_bayesiandenselayer_kernel(tc, x, w_loc, w_std, b_loc, b_std, eps_w, eps
         load_x(1, 1)
         load_loc(0)
         load_loc(1)
-        load_x(2, 0)
-        load_x(2, 1)
 
+        x_room((0, 1))
         grow(0)
-        sigmoid((0,))
+        fw[0] = f32p.tile([P, 2048], F32, name="fw0", tag="f", align_bytes=64)
+        for j in (0, 1024):
+            nc.scalar.activation(
+                out=fw[0][:, j:j + 1024], in_=flat(std[0])[:, j:j + 1024], func=ACT.Sigmoid, scale=-1.0
+            )
         x_half(0, 0, nc.vector.tensor_copy)
         grow(1)
         x_half(0, 1, nc.vector.tensor_copy)
         grow_eps(0)
         quant_x(0)
-        grow(2)
-        grow_eps(1)
-        grow(3)
-        grow_eps(2)
-        grow(4)
-        grow_eps(3)
-        grow_eps(4)
-        sigmoid((1, 2, 3))
-        ln((0, 1, 2, 3))
+        for i in range(2, 6):
+            grow(i)
+            grow_eps(i - 1)
+        grow_eps(5)
+        sigmoid((1, 2, 3, 4, 5))
+        ln((0, 1, 2, 3, 4, 5))
 
+        load_x(2, 0)
+        load_x(2, 1)
         load_x(3, 0)
         load_x(3, 1)
+        x_room((2, 3))
         psb = psum.tile([P, P], BF16, name="psb", tag="bank")
         nc.tensor.transpose(psb[:], zt[:], identb[:])
+        for i in (6, 7):
+            load_std(i)
+            load_eps(i)
         for c in (1, 2, 3):
             for h in range(2):
                 x_half(c, h, nc.scalar.copy)
-        load_std(6)
-        load_std(7)
+            if c < 3:
+                sigmoid((c + 5,))
         load_loc(2)
         load_loc(3)
+        for i in (8, 9, 10, 11):
+            load_std(i)
 
         bT = const.tile([P, 48], F32, name="bT")
         bl = const.tile([P, 16], F32, name="bl")
@@ -217,13 +231,15 @@ def tile_bayesiandenselayer_kernel(tc, x, w_loc, w_std, b_loc, b_std, eps_w, eps
             )
             nc.vector.tensor_tensor(out=bt[:], in0=bs[:], in1=bT[:, 32:48], op=ALU.mult)
             nc.vector.tensor_tensor(out=b16[:], in0=bt[:], in1=bT[:, 0:16], op=ALU.add)
+
+        def spread_bias():
             pb = psum.tile([P, 256], F32, name="pb", tag="bank")
             for s in range(2):
                 nc.tensor.matmul(
                     out=pb[:, s * P:(s + 1) * P], lhsT=b16[:, 14 + s:15 + s].to_broadcast([P, P]), rhs=ident[:],
                     start=True, stop=True,
                 )
-            return pb
+            nc.scalar.copy(out=bias_bc[:], in_=pb[:])
 
         def codes_of(first, c):
             n = len(pieces(first)[2])
@@ -284,50 +300,40 @@ def tile_bayesiandenselayer_kernel(tc, x, w_loc, w_std, b_loc, b_std, eps_w, eps
                 stop=(c == 3),
             )
 
-        def pair_steps(q):
+        def pair_steps(q, between=()):
             pair = (2 * q, 2 * q + 1)
             for i in pair:
                 times_eps(i)
                 load_eps(i + EPS_BUFS)
+            for step in between:
+                step()
             for i in pair:
                 plus_loc(i)
                 load_loc(i + LOC_BUFS)
             for i in pair:
                 quantise(i)
-            if q == 0:
-                grow(5)
-                grow_eps(5)
-            elif q < 6:
+            if q < 5:
                 for i in pair:
-                    grow(i + 4)
+                    grow(i + 6)
                 for i in pair:
-                    grow_eps(i + 4)
+                    grow_eps(i + 6)
 
         pair_steps(0)
         nc.vector.tensor_copy(out=bT[:], in_=psb[:, 0:48])
-        sigmoid((4, 5, 6, 7))
         nc.scalar.activation(out=bl[:], in_=bT[:, 16:32], func=ACT.Sigmoid, scale=-1.0)
-        nc.scalar.activation(out=bl[:], in_=bl[:], func=ACT.Ln, bias=TINY)
-        ln((4, 5, 6, 7))
-        load_std(8)
-        load_std(9)
-        load_std(10)
-        load_std(11)
-        pair_steps(1)
         load_std(12)
         load_std(13)
-        for c in (1, 2, 3):
-            quant_x(c)
-        pb = bias_finish()
+        pair_steps(1, between=[lambda c=c: quant_x(c) for c in (1, 2)])
+        quant_x(3)
         sigmoid((8, 9, 10, 11))
-        nc.scalar.copy(out=bias_bc[:], in_=pb[:])
-        pair_steps(2)
         load_std(14)
         load_std(15)
+        pair_steps(2)
         sigmoid((12, 13, 14, 15))
+        ln((6, 7))
+        nc.scalar.activation(out=bl[:], in_=bl[:], func=ACT.Ln, bias=TINY)
         ln((8, 9))
-        block_out(0)
-        pair_steps(3)
+        pair_steps(3, between=(bias_finish, lambda: block_out(0)))
         ln((10, 11))
         block_back(0)
         pair_steps(4)
@@ -336,16 +342,19 @@ def tile_bayesiandenselayer_kernel(tc, x, w_loc, w_std, b_loc, b_std, eps_w, eps
         pair_steps(5)
         ln((14, 15))
         block_back(4)
+        spread_bias()
         block_out(8)
-        pair_steps(6)
         block_back(8)
+        block_out(10)
+        block_back(10)
+        pair_steps(6)
         block_out(12)
         block_back(12)
 
         times_eps(14)
         times_eps(15)
         plus_loc(14)
-        plus_loc(15, parts=(0, 1, 2))
+        plus_loc(15, parts=(0,))
         quantise(14)
         acc14 = []
         for mh in range(2):
@@ -354,6 +363,7 @@ def tile_bayesiandenselayer_kernel(tc, x, w_loc, w_std, b_loc, b_std, eps_w, eps
                 for c in range(4):
                     direct_pass(14, c, 4 * mh + m4, t[:, m4, :])
             acc14.append(t)
+        plus_loc(15, parts=(1, 2))
         quantise(15, 0, 256)
         acc15 = {}
         for m in range(6):

@@ -16,9 +16,7 @@ P = 128
 CLAMP = 32.0
 TINY = 2.0 ** -63
 TILES = 16
-EPS_BUFS = 8
-STD_BUFS = 6
-LOC_BUFS = 4
+IN_BUFS = 18
 
 
 def tile_bayesiandenselayer_kernel(tc, x, w_loc, w_std, b_loc, b_std, eps_w, eps_b, out):
@@ -26,9 +24,7 @@ def tile_bayesiandenselayer_kernel(tc, x, w_loc, w_std, b_loc, b_std, eps_w, eps
     with ExitStack() as ctx:
         const = ctx.enter_context(tc.tile_pool(name="const", bufs=1))
         f32p = ctx.enter_context(tc.tile_pool(name="f32p", bufs=11))
-        stdp = ctx.enter_context(tc.tile_pool(name="stdp", bufs=STD_BUFS))
-        epsp = ctx.enter_context(tc.tile_pool(name="epsp", bufs=EPS_BUFS))
-        locp = ctx.enter_context(tc.tile_pool(name="locp", bufs=LOC_BUFS))
+        inp = ctx.enter_context(tc.tile_pool(name="inp", bufs=IN_BUFS))
         wbp = ctx.enter_context(tc.tile_pool(name="wbp", bufs=2))
         wcp = ctx.enter_context(tc.tile_pool(name="wcp", bufs=6))
         otp = ctx.enter_context(tc.tile_pool(name="otp", bufs=8))
@@ -47,17 +43,13 @@ def tile_bayesiandenselayer_kernel(tc, x, w_loc, w_std, b_loc, b_std, eps_w, eps
         std, eps, loc, fw, wb, wc, wp, gr = {}, {}, {}, {}, {}, {}, {}, {}
 
         def pieces(i):
-            if i < 8:
+            if i < 12:
                 return 512 * (i // 4), 512, (i % 4,)
-            if i < 14:
-                return 256 * (i // 2), 256, (2 * (i % 2), 2 * (i % 2) + 1)
-            return 1792 + 128 * (i - 14), 128, (0, 1, 2, 3)
+            return 256 * (i // 2), 256, (2 * (i % 2), 2 * (i % 2) + 1)
 
-        def load(pool, tag, store, src, i):
-            if i >= TILES:
-                return
+        def load(store, src, tag, i):
             col, wid, cs = pieces(i)
-            t = pool.tile([P, 4 * len(cs), wid], BF16, name="%s%d" % (tag, i), tag=tag)
+            t = inp.tile([P, 4 * len(cs), wid], BF16, name="%s%d" % (tag, i), tag="in")
             for s, c in enumerate(cs):
                 nc.sync.dma_start(
                     out=t[:, 4 * s:4 * s + 4, :],
@@ -66,13 +58,13 @@ def tile_bayesiandenselayer_kernel(tc, x, w_loc, w_std, b_loc, b_std, eps_w, eps
             store[i] = t
 
         def load_std(i):
-            load(stdp, "std", std, w_std, i)
+            load(std, w_std, "std", i)
 
         def load_eps(i):
-            load(epsp, "eps", eps, eps_w, i)
+            load(eps, eps_w, "eps", i)
 
         def load_loc(i):
-            load(locp, "loc", loc, w_loc, i)
+            load(loc, w_loc, "loc", i)
 
         def flat(t):
             return t[:].rearrange("p j n -> p (j n)")
@@ -100,12 +92,11 @@ def tile_bayesiandenselayer_kernel(tc, x, w_loc, w_std, b_loc, b_std, eps_w, eps
                 out=fw[i][:], in0=fw[i][:], scalar=-CLAMP, in1=flat(eps[i]), op0=ALU.max, op1=ALU.mult
             )
 
-        def plus_loc(i, parts=None):
+        def plus_loc(i):
             cs = pieces(i)[2]
             n = 2048 // len(cs)
-            if i not in wb:
-                wb[i] = wbp.tile([P, 2048], BF16, name="wb%d" % i, tag="wb", align_bytes=64)
-            for s in (range(len(cs)) if parts is None else parts):
+            wb[i] = wbp.tile([P, 2048], BF16, name="wb%d" % i, tag="wb", align_bytes=64)
+            for s in range(len(cs)):
                 nc.vector.tensor_tensor(
                     out=wb[i][:, s * n:(s + 1) * n].rearrange("p (cc i t) -> p cc t i", i=8, t=4),
                     in0=fw[i][:, s * n:(s + 1) * n].rearrange("p (t cc i) -> p cc t i", t=4, i=8),
@@ -128,8 +119,7 @@ def tile_bayesiandenselayer_kernel(tc, x, w_loc, w_std, b_loc, b_std, eps_w, eps
         xh = {}
 
         def load_x(c, h):
-            pool, tag = ((locp, "loc"), (locp, "loc"), (stdp, "std"), (stdp, "std"))[c]
-            t = pool.tile([P, 4, 512], BF16, name="x%d_%d" % (c, h), tag=tag)
+            t = inp.tile([P, 4, 512], BF16, name="x%d_%d" % (c, h), tag="in")
             nc.sync.dma_start(out=t[:], in_=xr[:, 4 * h:4 * h + 4, c * 512:(c + 1) * 512])
             xh[(c, h)] = t
 
@@ -155,31 +145,34 @@ def tile_bayesiandenselayer_kernel(tc, x, w_loc, w_std, b_loc, b_std, eps_w, eps
                 dst = xg[c][:].rearrange("p (m u) -> p m u", u=2)[:, rp * 256:(rp + 1) * 256, :]
                 copy(out=dst, in_=ps[:].rearrange("p u m -> p m u"))
 
-        std[0] = stdp.tile([P, 4, 512], BF16, name="std0", tag="std")
+        def load_bias():
+            for k, vec in enumerate((b_loc, b_std, eps_b)):
+                nc.sync.dma_start(out=zt[16 * k:16 * k + 16, :], in_=vec.rearrange("o (i p) -> (o i) p", p=P))
+
+        queue = []
+
+        def enlist(words):
+            for w in words.split():
+                kind, num = w[0], w[1:]
+                if kind == "b":
+                    queue.append(load_bias)
+                elif kind == "x":
+                    queue.append(lambda num=num: load_x(int(num[0]), int(num[1])))
+                else:
+                    queue.append(lambda kind=kind, num=num: {"s": load_std, "e": load_eps, "l": load_loc}[kind](int(num)))
+
+        def feed(n):
+            for step in queue[:n]:
+                step()
+            queue[:n] = []
+
+        std[0] = inp.tile([P, 4, 512], BF16, name="std0", tag="in")
         for j in (0, 2):
             nc.sync.dma_start(
                 out=std[0][:, j:j + 2, :], in_=w_std[0:512, 0:512].rearrange("(p j) n -> p j n", j=4)[:, j:j + 2, :]
             )
-        load_std(1)
-        load_x(0, 0)
-        load_std(2)
-        load_x(0, 1)
-        load_eps(0)
-        load_std(3)
-        load_eps(1)
-        load_std(4)
-        load_eps(2)
-        load_std(5)
-        load_eps(3)
-        load_eps(4)
-        for k, vec in enumerate((b_loc, b_std, eps_b)):
-            nc.sync.dma_start(out=zt[16 * k:16 * k + 16, :], in_=vec.rearrange("o (i p) -> (o i) p", p=P))
-        load_eps(5)
-        load_x(1, 0)
-        load_x(1, 1)
-        load_loc(0)
-        load_loc(1)
-
+        enlist("x00 s1 x01 s2 s3 e0 s4 e1 s5 e2 x10 x11 e3 e4 e5 b0 l0 l1 x20 x21 s6 s7 e6 e7 x30 x31 l2 l3 s8 s9 s10 s11 e8 e9 s12 s13 l4 l5 s14 s15 e10 e11 l6 l7 e12 e13 l8 l9 e14 e15 l10 l11 l12 l13 l14 l15")
+        feed(18)
         x_room((0, 1))
         grow(0)
         fw[0] = f32p.tile([P, 2048], F32, name="fw0", tag="f", align_bytes=64)
@@ -187,11 +180,11 @@ def tile_bayesiandenselayer_kernel(tc, x, w_loc, w_std, b_loc, b_std, eps_w, eps
             nc.scalar.activation(
                 out=fw[0][:, j:j + 1024], in_=flat(std[0])[:, j:j + 1024], func=ACT.Sigmoid, scale=-1.0
             )
-        x_half(0, 0, nc.vector.tensor_copy)
         grow(1)
+        x_half(0, 0, nc.vector.tensor_copy)
         x_half(0, 1, nc.vector.tensor_copy)
-        grow_eps(0)
         quant_x(0)
+        grow_eps(0)
         for i in range(2, 6):
             grow(i)
             grow_eps(i - 1)
@@ -199,25 +192,16 @@ def tile_bayesiandenselayer_kernel(tc, x, w_loc, w_std, b_loc, b_std, eps_w, eps
         sigmoid((1, 2, 3, 4, 5))
         ln((0, 1, 2, 3, 4, 5))
 
-        load_x(2, 0)
-        load_x(2, 1)
-        load_x(3, 0)
-        load_x(3, 1)
+        feed(8)
         x_room((2, 3))
         psb = psum.tile([P, P], BF16, name="psb", tag="bank")
         nc.tensor.transpose(psb[:], zt[:], identb[:])
-        for i in (6, 7):
-            load_std(i)
-            load_eps(i)
         for c in (1, 2, 3):
             for h in range(2):
                 x_half(c, h, nc.scalar.copy)
+                feed(1)
             if c < 3:
                 sigmoid((c + 5,))
-        load_loc(2)
-        load_loc(3)
-        for i in (8, 9, 10, 11):
-            load_std(i)
 
         bT = const.tile([P, 48], F32, name="bT")
         bl = const.tile([P, 16], F32, name="bl")
@@ -249,27 +233,40 @@ def tile_bayesiandenselayer_kernel(tc, x, w_loc, w_std, b_loc, b_std, eps_w, eps
 
         ot = {}
 
-        def block_out(first):
-            col, wid = pieces(first)[0:2]
-            for mh in range(2):
-                for nt in range(wid // P):
-                    at = psum.tile([P, 512], F32, name="at%d_%d_%d" % (first, nt, mh), tag="bank")
-                    for c in range(4):
-                        words, plane, off = codes_of(first, c)
-                        nc.tensor.matmul_mx(
-                            out=at[:],
-                            lhsT=words[:, off + nt * P:off + (nt + 1) * P].bitcast(FP8X4),
-                            lhsT_scale=plane[:, off + nt * P:off + (nt + 1) * P],
-                            rhs=x_codes[:, c, mh * 512:(mh + 1) * 512].bitcast(FP8X4),
-                            rhs_scale=x_scales[:, c, mh * 512:(mh + 1) * 512],
-                            start=(c == 0),
-                            stop=(c == 3),
-                        )
-                    ot[(nt, mh)] = otp.tile([P, 512], F32, name="ot%d_%d_%d" % (first, nt, mh), tag="ot")
-                    nc.scalar.activation(
-                        out=ot[(nt, mh)][:], in_=at[:], func=ACT.Identity,
-                        bias=b16[:, col // P + nt:col // P + nt + 1], scale=1.0,
+        at = {}
+
+        def groups_of(first):
+            return [(mh, nt) for mh in range(2) for nt in range(pieces(first)[1] // P)]
+
+        def multiply(first, groups, cs):
+            for mh, nt in groups:
+                if cs[0] == 0:
+                    at[(mh, nt)] = psum.tile([P, 512], F32, name="at%d_%d_%d" % (first, nt, mh), tag="bank")
+                for c in cs:
+                    words, plane, off = codes_of(first, c)
+                    nc.tensor.matmul_mx(
+                        out=at[(mh, nt)][:],
+                        lhsT=words[:, off + nt * P:off + (nt + 1) * P].bitcast(FP8X4),
+                        lhsT_scale=plane[:, off + nt * P:off + (nt + 1) * P],
+                        rhs=x_codes[:, c, mh * 512:(mh + 1) * 512].bitcast(FP8X4),
+                        rhs_scale=x_scales[:, c, mh * 512:(mh + 1) * 512],
+                        start=(c == 0),
+                        stop=(c == 3),
                     )
+
+        def add_bias(first, groups):
+            for mh, nt in groups:
+                ot[(nt, mh)] = otp.tile([P, 512], F32, name="ot%d_%d_%d" % (first, nt, mh), tag="ot")
+                nt16 = pieces(first)[0] // P + nt
+                nc.scalar.activation(
+                    out=ot[(nt, mh)][:], in_=at[(mh, nt)][:], func=ACT.Identity, bias=b16[:, nt16:nt16 + 1], scale=1.0
+                )
+
+        def block_out(first):
+            groups = groups_of(first)
+            for g in groups:
+                multiply(first, [g], (0, 1, 2, 3))
+                add_bias(first, [g])
 
         def block_back(first):
             col, wid = pieces(first)[0:2]
@@ -289,27 +286,38 @@ def tile_bayesiandenselayer_kernel(tc, x, w_loc, w_std, b_loc, b_std, eps_w, eps
                     in_=ost[:],
                 )
 
-        def direct_pass(i, c, m, acc):
+        def direct_pass(h, c, m, acc):
             nc.tensor.matmul_mx(
                 out=acc,
                 lhsT=x_codes[:, c, m * P:(m + 1) * P].bitcast(FP8X4),
                 lhsT_scale=x_scales[:, c, m * P:(m + 1) * P],
-                rhs=wc[i][:, c * P:(c + 1) * P].bitcast(FP8X4),
-                rhs_scale=wp[i][:, c * P:(c + 1) * P],
+                rhs=wc[14 + h][:, c * P:(c + 1) * P].bitcast(FP8X4),
+                rhs_scale=wp[14 + h][:, c * P:(c + 1) * P],
                 start=(c == 0),
                 stop=(c == 3),
+            )
+
+        def plus_loc_half(h, c):
+            if 14 + h not in wb:
+                wb[14 + h] = wbp.tile([P, 2048], BF16, name="wb%d" % (14 + h), tag="wb", align_bytes=64)
+            i, s = 14 + c // 2, c % 2
+            nc.vector.tensor_tensor(
+                out=wb[14 + h][:, 512 * c:512 * (c + 1)].rearrange("p (cc i t) -> p cc t i", i=8, t=4),
+                in0=fw[i][:, 1024 * s:1024 * (s + 1)].rearrange("p (t hh cc i) -> p hh cc t i", t=4, hh=2, i=8)[:, h],
+                in1=loc[i][:, 4 * s:4 * s + 4, P * h:P * (h + 1)].rearrange("p t (cc i) -> p cc t i", i=8),
+                op=ALU.add,
             )
 
         def pair_steps(q, between=()):
             pair = (2 * q, 2 * q + 1)
             for i in pair:
                 times_eps(i)
-                load_eps(i + EPS_BUFS)
+                feed(1)
             for step in between:
                 step()
             for i in pair:
                 plus_loc(i)
-                load_loc(i + LOC_BUFS)
+                feed(1)
             for i in pair:
                 quantise(i)
             if q < 5:
@@ -319,63 +327,71 @@ def tile_bayesiandenselayer_kernel(tc, x, w_loc, w_std, b_loc, b_std, eps_w, eps
                     grow_eps(i + 6)
 
         pair_steps(0)
+        feed(2)
         nc.vector.tensor_copy(out=bT[:], in_=psb[:, 0:48])
         nc.scalar.activation(out=bl[:], in_=bT[:, 16:32], func=ACT.Sigmoid, scale=-1.0)
-        load_std(12)
-        load_std(13)
         pair_steps(1, between=[lambda c=c: quant_x(c) for c in (1, 2)])
         quant_x(3)
         sigmoid((8, 9, 10, 11))
-        load_std(14)
-        load_std(15)
+        feed(2)
         pair_steps(2)
+        feed(2)
         sigmoid((12, 13, 14, 15))
         ln((6, 7))
         nc.scalar.activation(out=bl[:], in_=bl[:], func=ACT.Ln, bias=TINY)
         ln((8, 9))
         pair_steps(3, between=(bias_finish, lambda: block_out(0)))
+        feed(2)
         ln((10, 11))
         block_back(0)
         pair_steps(4)
+        feed(2)
         ln((12, 13))
         block_out(4)
-        pair_steps(5)
+        multiply(8, groups_of(8)[:4], (0, 1))
         ln((14, 15))
         block_back(4)
+        pair_steps(5)
         spread_bias()
-        block_out(8)
+        early = groups_of(8)[:4]
+        for g in early:
+            multiply(8, [g], (2, 3))
+            add_bias(8, [g])
+        for g in groups_of(8)[4:]:
+            multiply(8, [g], (0, 1, 2, 3))
+            add_bias(8, [g])
         block_back(8)
-        block_out(10)
-        block_back(10)
         pair_steps(6)
         block_out(12)
         block_back(12)
 
         times_eps(14)
         times_eps(15)
-        plus_loc(14)
-        plus_loc(15, parts=(0,))
+        for c in range(4):
+            plus_loc_half(0, c)
+        plus_loc_half(1, 0)
         quantise(14)
         acc14 = []
         for mh in range(2):
             t = psum.tile([P, 4, P], F32, name="accA%d" % mh, tag="bank")
             for m4 in range(4):
                 for c in range(4):
-                    direct_pass(14, c, 4 * mh + m4, t[:, m4, :])
+                    direct_pass(0, c, 4 * mh + m4, t[:, m4, :])
             acc14.append(t)
-        plus_loc(15, parts=(1, 2))
+        plus_loc_half(1, 1)
+        plus_loc_half(1, 2)
         quantise(15, 0, 256)
         acc15 = {}
         for m in range(6):
             acc15[m] = psum.tile([P, P], F32, name="accB%d" % m, tag="bank")
         for c in (0, 1):
             for m in range(6):
-                direct_pass(15, c, m, acc15[m][:])
-        plus_loc(15, parts=(3,))
+                direct_pass(1, c, m, acc15[m][:])
+        plus_loc_half(1, 3)
         quantise(15, 256, 512)
         for c in (2, 3):
             for m in range(6):
-                direct_pass(15, c, m, acc15[m][:])
+                direct_pass(1, c, m, acc15[m][:])
 
         def store(ost, mh, col):
             nc.sync.dma_start(
@@ -391,7 +407,7 @@ def tile_bayesiandenselayer_kernel(tc, x, w_loc, w_std, b_loc, b_std, eps_w, eps
         for m in (6, 7):
             acc15[m] = psum.tile([P, P], F32, name="accB%d" % m, tag="bank")
             for c in range(4):
-                direct_pass(15, c, m, acc15[m][:])
+                direct_pass(1, c, m, acc15[m][:])
         for mh in range(2):
             ost = ostp.tile([P, 4, P], F32, name="ostB%d" % mh, tag="ost")
             for m4 in range(4):

@@ -171,7 +171,7 @@ def tile_bayesiandenselayer_kernel(tc, x, w_loc, w_std, b_loc, b_std, eps_w, eps
             nc.sync.dma_start(
                 out=std[0][:, j:j + 2, :], in_=w_std[0:512, 0:512].rearrange("(p j) n -> p j n", j=4)[:, j:j + 2, :]
             )
-        enlist("x00 s1 x01 s2 s3 e0 s4 e1 s5 e2 x10 x11 e3 e4 e5 b0 l0 l1 x20 x21 s6 s7 e6 e7 x30 x31 l2 l3 s8 s9 s10 s11 e8 e9 s12 s13 l4 l5 s14 s15 e10 e11 l6 l7 e12 e13 l8 l9 e14 e15 l10 l11 l12 l13 l14 l15")
+        enlist("s1 x00 s2 x01 s3 e0 s4 s5 e1 e2 e3 e4 b0 l0 l1 e5 x10 x11 x20 x21 s6 s7 e6 e7 x30 x31 l2 l3 s8 s9 s10 s11 e8 e9 s12 s13 l4 l5 s14 s15 e10 e11 l6 l7 e12 e13 l8 l9 e14 e15 l10 l11 l12 l13 l14 l15")
         feed(18)
         x_room((0, 1))
         grow(0)
@@ -180,17 +180,20 @@ def tile_bayesiandenselayer_kernel(tc, x, w_loc, w_std, b_loc, b_std, eps_w, eps
             nc.scalar.activation(
                 out=fw[0][:, j:j + 1024], in_=flat(std[0])[:, j:j + 1024], func=ACT.Sigmoid, scale=-1.0
             )
-        grow(1)
         x_half(0, 0, nc.vector.tensor_copy)
+        grow(1)
         x_half(0, 1, nc.vector.tensor_copy)
         quant_x(0)
         grow_eps(0)
-        for i in range(2, 6):
-            grow(i)
-            grow_eps(i - 1)
-        grow_eps(5)
-        sigmoid((1, 2, 3, 4, 5))
-        ln((0, 1, 2, 3, 4, 5))
+        grow(2)
+        grow_eps(1)
+        grow(3)
+        grow_eps(2)
+        grow(4)
+        grow_eps(3)
+        grow_eps(4)
+        sigmoid(range(1, 6))
+        ln(range(0, 6))
 
         feed(8)
         x_room((2, 3))
@@ -308,7 +311,14 @@ def tile_bayesiandenselayer_kernel(tc, x, w_loc, w_std, b_loc, b_std, eps_w, eps
                 op=ALU.add,
             )
 
-        def pair_steps(q, between=()):
+        def guard(tiles):
+            for i in range(0, len(tiles), 2):
+                for j in tiles[i:i + 2]:
+                    grow(j)
+                for j in tiles[i:i + 2]:
+                    grow_eps(j)
+
+        def pair_steps(q, between=(), ahead=()):
             pair = (2 * q, 2 * q + 1)
             for i in pair:
                 times_eps(i)
@@ -320,31 +330,27 @@ def tile_bayesiandenselayer_kernel(tc, x, w_loc, w_std, b_loc, b_std, eps_w, eps
                 feed(1)
             for i in pair:
                 quantise(i)
-            if q < 5:
-                for i in pair:
-                    grow(i + 6)
-                for i in pair:
-                    grow_eps(i + 6)
+            guard(ahead)
 
-        pair_steps(0)
+        pair_steps(0, ahead=(5, 6, 7))
         feed(2)
         nc.vector.tensor_copy(out=bT[:], in_=psb[:, 0:48])
         nc.scalar.activation(out=bl[:], in_=bT[:, 16:32], func=ACT.Sigmoid, scale=-1.0)
-        pair_steps(1, between=[lambda c=c: quant_x(c) for c in (1, 2)])
+        pair_steps(1, ahead=(8, 9), between=[lambda c=c: quant_x(c) for c in (1, 2)])
         quant_x(3)
-        sigmoid((8, 9, 10, 11))
+        sigmoid(range(8, 12))
         feed(2)
-        pair_steps(2)
+        pair_steps(2, ahead=(10, 11))
         feed(2)
-        sigmoid((12, 13, 14, 15))
-        ln((6, 7))
+        sigmoid(range(12, 16))
+        ln(range(6, 8))
         nc.scalar.activation(out=bl[:], in_=bl[:], func=ACT.Ln, bias=TINY)
         ln((8, 9))
-        pair_steps(3, between=(bias_finish, lambda: block_out(0)))
+        pair_steps(3, ahead=(12, 13), between=(bias_finish, lambda: block_out(0)))
         feed(2)
         ln((10, 11))
         block_back(0)
-        pair_steps(4)
+        pair_steps(4, ahead=(14, 15))
         feed(2)
         ln((12, 13))
         block_out(4)

@@ -171,7 +171,7 @@ def tile_bayesiandenselayer_kernel(tc, x, w_loc, w_std, b_loc, b_std, eps_w, eps
             nc.sync.dma_start(
                 out=std[0][:, j:j + 2, :], in_=w_std[0:512, 0:512].rearrange("(p j) n -> p j n", j=4)[:, j:j + 2, :]
             )
-        enlist("s1 x00 s2 x01 s3 e0 s4 s5 e1 e2 e3 e4 b0 l0 l1 e5 x10 x11 x20 x21 s6 s7 e6 e7 x30 x31 l2 l3 s8 s9 s10 s11 e8 e9 s12 s13 l4 l5 s14 s15 e10 e11 l6 l7 e12 e13 l8 l9 e14 e15 l10 l11 l12 l13 l14 l15")
+        enlist("s1 x00 s2 x01 s3 e0 b0 s4 s5 e1 e2 e3 e4 l0 l1 e5 x10 x11 x20 x21 s6 s7 e6 e7 x30 x31 l2 l3 s8 s9 s10 s11 e8 e9 s12 s13 l4 l5 s14 s15 e10 e11 l6 l7 e12 e13 l8 l9 e14 e15 l10 l11 l12 l13 l14 l15")
         feed(18)
         x_room((0, 1))
         grow(0)
@@ -192,13 +192,23 @@ def tile_bayesiandenselayer_kernel(tc, x, w_loc, w_std, b_loc, b_std, eps_w, eps
         grow(4)
         grow_eps(3)
         grow_eps(4)
+        bT = const.tile([P, 48], F32, name="bT")
+        bl = const.tile([P, 16], F32, name="bl")
+        bs = const.tile([P, 16], F32, name="bs")
+        bt = const.tile([P, 16], F32, name="bt")
+        b16 = const.tile([P, 16], F32, name="b16")
+
+        psb = psum.tile([P, P], BF16, name="psb", tag="bank")
+        nc.tensor.transpose(psb[:], zt[:], identb[:])
         sigmoid(range(1, 6))
-        ln(range(0, 6))
+        nc.scalar.copy(out=bT[:], in_=psb[:, 0:48])
+        nc.scalar.activation(out=bl[:], in_=bT[:, 16:32], func=ACT.Sigmoid, scale=-1.0)
+        ln((0, 1))
+        nc.scalar.activation(out=bl[:], in_=bl[:], func=ACT.Ln, bias=TINY)
+        ln(range(2, 6))
 
         feed(8)
         x_room((2, 3))
-        psb = psum.tile([P, P], BF16, name="psb", tag="bank")
-        nc.tensor.transpose(psb[:], zt[:], identb[:])
         for c in (1, 2, 3):
             for h in range(2):
                 x_half(c, h, nc.scalar.copy)
@@ -206,18 +216,15 @@ def tile_bayesiandenselayer_kernel(tc, x, w_loc, w_std, b_loc, b_std, eps_w, eps
             if c < 3:
                 sigmoid((c + 5,))
 
-        bT = const.tile([P, 48], F32, name="bT")
-        bl = const.tile([P, 16], F32, name="bl")
-        bs = const.tile([P, 16], F32, name="bs")
-        bt = const.tile([P, 16], F32, name="bt")
-        b16 = const.tile([P, 16], F32, name="b16")
-
-        def bias_finish():
-            nc.vector.scalar_tensor_tensor(
-                out=bs[:], in0=bl[:], scalar=-1.0, in1=bT[:, 16:32], op0=ALU.mult, op1=ALU.max
-            )
-            nc.vector.tensor_tensor(out=bt[:], in0=bs[:], in1=bT[:, 32:48], op=ALU.mult)
-            nc.vector.tensor_tensor(out=b16[:], in0=bt[:], in1=bT[:, 0:16], op=ALU.add)
+        def bias_step(n):
+            if n == 0:
+                nc.vector.scalar_tensor_tensor(
+                    out=bs[:], in0=bl[:], scalar=-1.0, in1=bT[:, 16:32], op0=ALU.mult, op1=ALU.max
+                )
+            elif n == 1:
+                nc.vector.tensor_tensor(out=bt[:], in0=bs[:], in1=bT[:, 32:48], op=ALU.mult)
+            else:
+                nc.vector.tensor_tensor(out=b16[:], in0=bt[:], in1=bT[:, 0:16], op=ALU.add)
 
         def spread_bias():
             pb = psum.tile([P, 256], F32, name="pb", tag="bank")
@@ -334,9 +341,7 @@ def tile_bayesiandenselayer_kernel(tc, x, w_loc, w_std, b_loc, b_std, eps_w, eps
 
         pair_steps(0, ahead=(5, 6, 7))
         feed(2)
-        nc.vector.tensor_copy(out=bT[:], in_=psb[:, 0:48])
-        nc.scalar.activation(out=bl[:], in_=bT[:, 16:32], func=ACT.Sigmoid, scale=-1.0)
-        pair_steps(1, ahead=(8, 9), between=[lambda c=c: quant_x(c) for c in (1, 2)])
+        pair_steps(1, ahead=(8, 9), between=(lambda: bias_step(0), lambda: quant_x(1), lambda: bias_step(1), lambda: quant_x(2), lambda: bias_step(2)))
         quant_x(3)
         sigmoid(range(8, 12))
         feed(2)
@@ -344,9 +349,8 @@ def tile_bayesiandenselayer_kernel(tc, x, w_loc, w_std, b_loc, b_std, eps_w, eps
         feed(2)
         sigmoid(range(12, 16))
         ln(range(6, 8))
-        nc.scalar.activation(out=bl[:], in_=bl[:], func=ACT.Ln, bias=TINY)
         ln((8, 9))
-        pair_steps(3, ahead=(12, 13), between=(bias_finish, lambda: block_out(0)))
+        pair_steps(3, ahead=(12, 13), between=(lambda: block_out(0),))
         feed(2)
         ln((10, 11))
         block_back(0)
@@ -378,6 +382,19 @@ def tile_bayesiandenselayer_kernel(tc, x, w_loc, w_std, b_loc, b_std, eps_w, eps
         plus_loc_half(1, 0)
         quantise(14)
         acc14 = []
+
+        def store(ost, m, n, col):
+            nc.sync.dma_start(
+                out=out[m * P:(m + n) * P, col:col + P].rearrange("(m p) n -> p m n", p=P), in_=ost[:]
+            )
+
+        def leave_a(mh):
+            ost = ostp.tile([P, 4, P], F32, name="ostA%d" % mh, tag="ost")
+            nc.vector.tensor_tensor(
+                out=ost[:], in0=acc14[mh][:], in1=bias_bc[:, 0:P].unsqueeze(1).to_broadcast([P, 4, P]), op=ALU.add
+            )
+            store(ost, 4 * mh, 4, 1792)
+
         for mh in range(2):
             t = psum.tile([P, 4, P], F32, name="accA%d" % mh, tag="bank")
             for m4 in range(4):
@@ -394,30 +411,21 @@ def tile_bayesiandenselayer_kernel(tc, x, w_loc, w_std, b_loc, b_std, eps_w, eps
             for m in range(6):
                 direct_pass(1, c, m, acc15[m][:])
         plus_loc_half(1, 3)
+        leave_a(0)
         quantise(15, 256, 512)
         for c in (2, 3):
             for m in range(6):
                 direct_pass(1, c, m, acc15[m][:])
+        leave_a(1)
 
-        def store(ost, mh, col):
-            nc.sync.dma_start(
-                out=out[4 * mh * P:(4 * mh + 4) * P, col:col + P].rearrange("(m p) n -> p m n", p=P), in_=ost[:]
-            )
-
-        for mh in range(2):
-            ost = ostp.tile([P, 4, P], F32, name="ostA%d" % mh, tag="ost")
-            nc.vector.tensor_tensor(
-                out=ost[:], in0=acc14[mh][:], in1=bias_bc[:, 0:P].unsqueeze(1).to_broadcast([P, 4, P]), op=ALU.add
-            )
-            store(ost, mh, 1792)
         for m in (6, 7):
             acc15[m] = psum.tile([P, P], F32, name="accB%d" % m, tag="bank")
             for c in range(4):
                 direct_pass(1, c, m, acc15[m][:])
-        for mh in range(2):
-            ost = ostp.tile([P, 4, P], F32, name="ostB%d" % mh, tag="ost")
-            for m4 in range(4):
+        for mb in range(4):
+            ost = ostp.tile([P, 2, P], F32, name="ostB%d" % mb, tag="ost")
+            for m2 in range(2):
                 nc.vector.tensor_tensor(
-                    out=ost[:, m4, :], in0=acc15[4 * mh + m4][:], in1=bias_bc[:, P:2 * P], op=ALU.add
+                    out=ost[:, m2, :], in0=acc15[2 * mb + m2][:], in1=bias_bc[:, P:2 * P], op=ALU.add
                 )
-            store(ost, mh, 1920)
+            store(ost, 2 * mb, 2, 1920)

from contextlib import ExitStack

import concourse.mybir as mybir
from concourse.masks import make_identity

FLOPS = 2 * 1024 * 2048 * 2048

F32 = mybir.dt.float32
BF16 = mybir.dt.bfloat16
U32 = mybir.dt.uint32
U8 = mybir.dt.uint8
FP8X4 = mybir.dt.float8_e4m3fn_x4
ACT = mybir.ActivationFunctionType
ALU = mybir.AluOpType
P = 128
CLAMP = 32.0
TINY = 2.0 ** -63
TILES = 16
IN_BUFS = 18


def tile_bayesiandenselayer_kernel(tc, x, w_loc, w_std, b_loc, b_std, eps_w, eps_b, out):
    nc = tc.nc
    with ExitStack() as ctx:
        const = ctx.enter_context(tc.tile_pool(name="const", bufs=1))
        f32p = ctx.enter_context(tc.tile_pool(name="f32p", bufs=11))
        inp = ctx.enter_context(tc.tile_pool(name="inp", bufs=IN_BUFS))
        wbp = ctx.enter_context(tc.tile_pool(name="wbp", bufs=2))
        wcp = ctx.enter_context(tc.tile_pool(name="wcp", bufs=6))
        otp = ctx.enter_context(tc.tile_pool(name="otp", bufs=8))
        ostp = ctx.enter_context(tc.tile_pool(name="ostp", bufs=8))
        psum = ctx.enter_context(tc.psum_pool(name="psum", bufs=8))
        ctx.enter_context(tc.manual_schedule())

        ident = const.tile([P, P], F32, name="ident")
        identb = const.tile([P, P], BF16, name="identb")
        make_identity(nc, ident[:])
        make_identity(nc, identb[:])
        bias_bc = const.tile([P, 256], F32, name="bias_bc")
        x_codes = const.tile([P, 4, 1024], U32, name="x_codes", align_bytes=64)
        x_scales = const.tile([P, 4, 1024], U8, name="x_scales", align_bytes=64)

        std, eps, loc, fw, wb, wc, wp, gr = {}, {}, {}, {}, {}, {}, {}, {}

        def pieces(i):
            if i < 12:
                return 512 * (i // 4), 512, (i % 4,)
            return 256 * (i // 2), 256, (2 * (i % 2), 2 * (i % 2) + 1)

        def load(store, src, tag, i):
            col, wid, cs = pieces(i)
            t = inp.tile([P, 4 * len(cs), wid], BF16, name="%s%d" % (tag, i), tag="in")
            for s, c in enumerate(cs):
                nc.sync.dma_start(
                    out=t[:, 4 * s:4 * s + 4, :],
                    in_=src[c * 512:(c + 1) * 512, col:col + wid].rearrange("(p j) n -> p j n", j=4),
                )
            store[i] = t

        def load_std(i):
            load(std, w_std, "std", i)

        def load_eps(i):
            load(eps, eps_w, "eps", i)

        def load_loc(i):
            load(loc, w_loc, "loc", i)

        def flat(t):
            return t[:].rearrange("p j n -> p (j n)")

        def sigmoid(tiles):
            for i in tiles:
                fw[i] = f32p.tile([P, 2048], F32, name="fw%d" % i, tag="f", align_bytes=64)
                nc.scalar.activation(out=fw[i][:], in_=flat(std[i]), func=ACT.Sigmoid, scale=-1.0)

        def ln(tiles):
            for i in tiles:
                nc.scalar.activation(out=fw[i][:], in_=fw[i][:], func=ACT.Ln, bias=TINY)

        def grow(i):
            gr[i] = wbp.tile([P, 2048], BF16, name="gr%d" % i, tag="wb", align_bytes=64)
            nc.vector.tensor_scalar(
                out=gr[i][:], in0=flat(std[i]), scalar1=-1.0 / CLAMP, scalar2=-1.0, op0=ALU.mult, op1=ALU.min
            )

        def grow_eps(i):
            nc.vector.tensor_tensor(out=flat(eps[i]), in0=flat(eps[i]), in1=gr[i][:], op=ALU.mult)

        def times_eps(i):
            nc.vector.scalar_tensor_tensor(
                out=fw[i][:], in0=fw[i][:], scalar=-CLAMP, in1=flat(eps[i]), op0=ALU.max, op1=ALU.mult
            )

        def plus_loc(i):
            cs = pieces(i)[2]
            n = 2048 // len(cs)
            wb[i] = wbp.tile([P, 2048], BF16, name="wb%d" % i, tag="wb", align_bytes=64)
            for s in range(len(cs)):
                nc.vector.tensor_tensor(
                    out=wb[i][:, s * n:(s + 1) * n].rearrange("p (cc i t) -> p cc t i", i=8, t=4),
                    in0=fw[i][:, s * n:(s + 1) * n].rearrange("p (t cc i) -> p cc t i", t=4, i=8),
                    in1=loc[i][:, 4 * s:4 * s + 4, :].rearrange("p t (cc i) -> p cc t i", i=8),
                    op=ALU.add,
                )

        def quantise(i, lo=0, hi=512):
            if i not in wc:
                wc[i] = wcp.tile([P, 512], U32, name="wc%d" % i, tag="wc", align_bytes=64)
                wp[i] = wcp.tile([P, 512], U8, name="wp%d" % i, tag="wp", align_bytes=64)
            nc.vector.quantize_mx(
                out=wc[i][:, lo:hi].bitcast(FP8X4), scales=wp[i][:, lo:hi], in_=wb[i][:, 4 * lo:4 * hi]
            )

        zt = const.tile([P, P], BF16, name="zt")
        nc.vector.memset(zt[:], 0.0)

        xr = x.rearrange("(r p) k -> p r k", p=P)
        xh = {}

        def load_x(c, h):
            t = inp.tile([P, 4, 512], BF16, name="x%d_%d" % (c, h), tag="in")
            nc.sync.dma_start(out=t[:], in_=xr[:, 4 * h:4 * h + 4, c * 512:(c + 1) * 512])
            xh[(c, h)] = t

        xg = {}

        def x_room(cs):
            for c in cs:
                xg[c] = f32p.tile([P, 2048], F32, name="xg%d" % c, tag="f", align_bytes=64)

        def quant_x(c):
            nc.vector.quantize_mx(
                out=x_codes[:, c, :].bitcast(FP8X4), scales=x_scales[:, c, :], in_=xg[c][:].bitcast(BF16)
            )

        def x_half(c, h, copy):
            for rp in (2 * h, 2 * h + 1):
                ps = psum.tile([P, 2, 256], F32, name="xt%d_%d" % (c, rp), tag="bank")
                for r2 in range(2):
                    r = 2 * rp + r2
                    words = xh[(c, h)][:].bitcast(F32)[:, r % 4, :].rearrange("p (q u) -> p u q", u=2)
                    for u in range(2):
                        nc.tensor.transpose(ps[:, u, r2 * P:(r2 + 1) * P], words[:, u, :], ident[:])
                dst = xg[c][:].rearrange("p (m u) -> p m u", u=2)[:, rp * 256:(rp + 1) * 256, :]
                copy(out=dst, in_=ps[:].rearrange("p u m -> p m u"))

        def load_bias():
            for k, vec in enumerate((b_loc, b_std, eps_b)):
                nc.sync.dma_start(out=zt[16 * k:16 * k + 16, :], in_=vec.rearrange("o (i p) -> (o i) p", p=P))

        queue = []

        def enlist(words):
            for w in words.split():
                kind, num = w[0], w[1:]
                if kind == "b":
                    queue.append(load_bias)
                elif kind == "x":
                    queue.append(lambda num=num: load_x(int(num[0]), int(num[1])))
                else:
                    queue.append(lambda kind=kind, num=num: {"s": load_std, "e": load_eps, "l": load_loc}[kind](int(num)))

        def feed(n):
            for step in queue[:n]:
                step()
            queue[:n] = []

        std[0] = inp.tile([P, 4, 512], BF16, name="std0", tag="in")
        for j in (0, 2):
            nc.sync.dma_start(
                out=std[0][:, j:j + 2, :], in_=w_std[0:512, 0:512].rearrange("(p j) n -> p j n", j=4)[:, j:j + 2, :]
            )
        enlist("s1 x00 s2 x01 s3 e0 b0 s4 s5 e1 e2 e3 e4 l0 l1 e5 x10 x11 x20 x21 s6 s7 e6 e7 x30 x31 l2 l3 s8 s9 s10 s11 e8 e9 s12 s13 l4 l5 s14 s15 e10 e11 l6 l7 e12 e13 l8 l9 e14 e15 l10 l11 l12 l13 l14 l15")
        feed(18)
        x_room((0, 1))
        grow(0)
        fw[0] = f32p.tile([P, 2048], F32, name="fw0", tag="f", align_bytes=64)
        for j in (0, 1024):
            nc.scalar.activation(
                out=fw[0][:, j:j + 1024], in_=flat(std[0])[:, j:j + 1024], func=ACT.Sigmoid, scale=-1.0
            )
        x_half(0, 0, nc.vector.tensor_copy)
        grow(1)
        x_half(0, 1, nc.vector.tensor_copy)
        quant_x(0)
        grow_eps(0)
        grow(2)
        grow_eps(1)
        grow(3)
        grow_eps(2)
        grow(4)
        grow_eps(3)
        grow_eps(4)
        bT = const.tile([P, 48], F32, name="bT")
        bl = const.tile([P, 16], F32, name="bl")
        bs = const.tile([P, 16], F32, name="bs")
        bt = const.tile([P, 16], F32, name="bt")
        b16 = const.tile([P, 16], F32, name="b16")

        psb = psum.tile([P, P], BF16, name="psb", tag="bank")
        nc.tensor.transpose(psb[:], zt[:], identb[:])
        sigmoid(range(1, 6))
        nc.scalar.copy(out=bT[:], in_=psb[:, 0:48])
        nc.scalar.activation(out=bl[:], in_=bT[:, 16:32], func=ACT.Sigmoid, scale=-1.0)
        ln((0, 1))
        nc.scalar.activation(out=bl[:], in_=bl[:], func=ACT.Ln, bias=TINY)
        ln(range(2, 6))

        feed(8)
        x_room((2, 3))
        for c in (1, 2, 3):
            for h in range(2):
                x_half(c, h, nc.scalar.copy)
                feed(1)
            if c < 3:
                sigmoid((c + 5,))

        def bias_step(n):
            if n == 0:
                nc.vector.scalar_tensor_tensor(
                    out=bs[:], in0=bl[:], scalar=-1.0, in1=bT[:, 16:32], op0=ALU.mult, op1=ALU.max
                )
            elif n == 1:
                nc.vector.tensor_tensor(out=bt[:], in0=bs[:], in1=bT[:, 32:48], op=ALU.mult)
            else:
                nc.vector.tensor_tensor(out=b16[:], in0=bt[:], in1=bT[:, 0:16], op=ALU.add)

        def spread_bias():
            pb = psum.tile([P, 256], F32, name="pb", tag="bank")
            for s in range(2):
                nc.tensor.matmul(
                    out=pb[:, s * P:(s + 1) * P], lhsT=b16[:, 14 + s:15 + s].to_broadcast([P, P]), rhs=ident[:],
                    start=True, stop=True,
                )
            nc.scalar.copy(out=bias_bc[:], in_=pb[:])

        def codes_of(first, c):
            n = len(pieces(first)[2])
            i = first + c // n
            off = (c % n) * pieces(first)[1]
            return wc[i], wp[i], off

        ot = {}

        at = {}

        def groups_of(first):
            return [(mh, nt) for mh in range(2) for nt in range(pieces(first)[1] // P)]

        def multiply(first, groups, cs):
            for mh, nt in groups:
                if cs[0] == 0:
                    at[(mh, nt)] = psum.tile([P, 512], F32, name="at%d_%d_%d" % (first, nt, mh), tag="bank")
                for c in cs:
                    words, plane, off = codes_of(first, c)
                    nc.tensor.matmul_mx(
                        out=at[(mh, nt)][:],
                        lhsT=words[:, off + nt * P:off + (nt + 1) * P].bitcast(FP8X4),
                        lhsT_scale=plane[:, off + nt * P:off + (nt + 1) * P],
                        rhs=x_codes[:, c, mh * 512:(mh + 1) * 512].bitcast(FP8X4),
                        rhs_scale=x_scales[:, c, mh * 512:(mh + 1) * 512],
                        start=(c == 0),
                        stop=(c == 3),
                    )

        def add_bias(first, groups):
            for mh, nt in groups:
                ot[(nt, mh)] = otp.tile([P, 512], F32, name="ot%d_%d_%d" % (first, nt, mh), tag="ot")
                nt16 = pieces(first)[0] // P + nt
                nc.scalar.activation(
                    out=ot[(nt, mh)][:], in_=at[(mh, nt)][:], func=ACT.Identity, bias=b16[:, nt16:nt16 + 1], scale=1.0
                )

        def block_out(first):
            groups = groups_of(first)
            for g in groups:
                multiply(first, [g], (0, 1, 2, 3))
                add_bias(first, [g])

        def block_back(first):
            col, wid = pieces(first)[0:2]
            per = 512 // wid
            for mb in range(8 // per):
                tb = psum.tile([P, per, wid], F32, name="tb%d_%d" % (first, mb), tag="bank")
                for m2 in range(per):
                    m = mb * per + m2
                    for nt in range(wid // P):
                        nc.tensor.transpose(
                            tb[:, m2, nt * P:(nt + 1) * P], ot[(nt, m // 4)][:, (m % 4) * P:(m % 4 + 1) * P], ident[:]
                        )
                ost = ostp.tile([P, per, wid], F32, name="ost%d_%d" % (first, mb), tag="ost")
                nc.scalar.copy(out=ost[:], in_=tb[:])
                nc.sync.dma_start(
                    out=out[mb * per * P:(mb + 1) * per * P, col:col + wid].rearrange("(m2 p) n -> p m2 n", p=P),
                    in_=ost[:],
                )

        def direct_pass(h, c, m, acc):
            nc.tensor.matmul_mx(
                out=acc,
                lhsT=x_codes[:, c, m * P:(m + 1) * P].bitcast(FP8X4),
                lhsT_scale=x_scales[:, c, m * P:(m + 1) * P],
                rhs=wc[14 + h][:, c * P:(c + 1) * P].bitcast(FP8X4),
                rhs_scale=wp[14 + h][:, c * P:(c + 1) * P],
                start=(c == 0),
                stop=(c == 3),
            )

        def plus_loc_half(h, c):
            if 14 + h not in wb:
                wb[14 + h] = wbp.tile([P, 2048], BF16, name="wb%d" % (14 + h), tag="wb", align_bytes=64)
            i, s = 14 + c // 2, c % 2
            nc.vector.tensor_tensor(
                out=wb[14 + h][:, 512 * c:512 * (c + 1)].rearrange("p (cc i t) -> p cc t i", i=8, t=4),
                in0=fw[i][:, 1024 * s:1024 * (s + 1)].rearrange("p (t hh cc i) -> p hh cc t i", t=4, hh=2, i=8)[:, h],
                in1=loc[i][:, 4 * s:4 * s + 4, P * h:P * (h + 1)].rearrange("p t (cc i) -> p cc t i", i=8),
                op=ALU.add,
            )

        def guard(tiles):
            for i in range(0, len(tiles), 2):
                for j in tiles[i:i + 2]:
                    grow(j)
                for j in tiles[i:i + 2]:
                    grow_eps(j)

        def pair_steps(q, between=(), ahead=()):
            pair = (2 * q, 2 * q + 1)
            for i in pair:
                times_eps(i)
                feed(1)
            for step in between:
                step()
            for i in pair:
                plus_loc(i)
                feed(1)
            for i in pair:
                quantise(i)
            guard(ahead)

        pair_steps(0, ahead=(5, 6, 7))
        feed(2)
        pair_steps(1, ahead=(8, 9), between=(lambda: bias_step(0), lambda: quant_x(1), lambda: bias_step(1), lambda: quant_x(2), lambda: bias_step(2)))
        quant_x(3)
        sigmoid(range(8, 12))
        feed(2)
        pair_steps(2, ahead=(10, 11))
        feed(2)
        sigmoid(range(12, 16))
        ln(range(6, 8))
        ln((8, 9))
        pair_steps(3, ahead=(12, 13), between=(lambda: block_out(0),))
        feed(2)
        ln((10, 11))
        block_back(0)
        pair_steps(4, ahead=(14, 15))
        feed(2)
        ln((12, 13))
        block_out(4)
        multiply(8, groups_of(8)[:4], (0, 1))
        ln((14, 15))
        block_back(4)
        pair_steps(5)
        spread_bias()
        early = groups_of(8)[:4]
        for g in early:
            multiply(8, [g], (2, 3))
            add_bias(8, [g])
        for g in groups_of(8)[4:]:
            multiply(8, [g], (0, 1, 2, 3))
            add_bias(8, [g])
        block_back(8)
        pair_steps(6)
        block_out(12)
        block_back(12)

        times_eps(14)
        times_eps(15)
        for c in range(4):
            plus_loc_half(0, c)
        plus_loc_half(1, 0)
        quantise(14)
        acc14 = []

        def store(ost, m, n, col):
            nc.sync.dma_start(
                out=out[m * P:(m + n) * P, col:col + P].rearrange("(m p) n -> p m n", p=P), in_=ost[:]
            )

        def leave_a(mh):
            ost = ostp.tile([P, 4, P], F32, name="ostA%d" % mh, tag="ost")
            nc.vector.tensor_tensor(
                out=ost[:], in0=acc14[mh][:], in1=bias_bc[:, 0:P].unsqueeze(1).to_broadcast([P, 4, P]), op=ALU.add
            )
            store(ost, 4 * mh, 4, 1792)

        for mh in range(2):
            t = psum.tile([P, 4, P], F32, name="accA%d" % mh, tag="bank")
            for m4 in range(4):
                for c in range(4):
                    direct_pass(0, c, 4 * mh + m4, t[:, m4, :])
            acc14.append(t)
        plus_loc_half(1, 1)
        plus_loc_half(1, 2)
        quantise(15, 0, 256)
        acc15 = {}
        for m in range(6):
            acc15[m] = psum.tile([P, P], F32, name="accB%d" % m, tag="bank")
        for c in (0, 1):
            for m in range(6):
                direct_pass(1, c, m, acc15[m][:])
        plus_loc_half(1, 3)
        leave_a(0)
        quantise(15, 256, 512)
        for c in (2, 3):
            for m in range(6):
                direct_pass(1, c, m, acc15[m][:])
        leave_a(1)

        for m in (6, 7):
            acc15[m] = psum.tile([P, P], F32, name="accB%d" % m, tag="bank")
            for c in range(4):
                direct_pass(1, c, m, acc15[m][:])
        for mb in range(4):
            ost = ostp.tile([P, 2, P], F32, name="ostB%d" % mb, tag="ost")
            for m2 in range(2):
                nc.vector.tensor_tensor(
                    out=ost[:, m2, :], in0=acc15[2 * mb + m2][:], in1=bias_bc[:, P:2 * P], op=ALU.add
                )
            store(ost, 2 * mb, 2, 1920)
